import numpy as np
import ml_dtypes


def mxq(x, axis, fmt="e4m3"):
    dtype, down = {"e4m3": (ml_dtypes.float8_e4m3fn, 7), "e5m2": (ml_dtypes.float8_e5m2, 14)}[fmt]
    v = np.moveaxis(np.asarray(x, np.float32).astype(ml_dtypes.bfloat16).astype(np.float64), axis, -1)
    blocks = v.reshape(v.shape[:-1] + (-1, 32))
    amax = np.abs(blocks).max(-1, keepdims=True)
    byte = np.maximum(np.where(amax > 0, np.frexp(amax)[1] - 1 + 127, 0) - down, 1)
    scale = np.exp2(byte - 127.0)
    codes = (blocks / scale).astype(np.float32).astype(dtype).astype(np.float64)
    return np.moveaxis((codes * scale).reshape(v.shape), -1, axis)


WIDE = False


def mx_kscale(k):
    if not WIDE:
        return np.ones(k)
    levels = np.array([10, -10, 5, -5, 0])
    a = np.random.permutation(np.resize(levels, k // 512 * 4)).reshape(k // 512, 4)
    idx = np.arange(k)
    return np.exp2(a[idx // 512, idx % 128 // 32])


BF16 = ml_dtypes.bfloat16


def bf(x):
    return np.asarray(x, np.float32).astype(BF16)


def f64(x):
    return np.asarray(x).astype(np.float64)


E2M1 = np.array([0.0, 0.5, 1.0, 1.5, 2.0, 3.0, 4.0, 6.0, -0.0, -0.5, -1.0, -1.5, -2.0, -3.0, -4.0, -6.0])


def pack_weight(w, fmt):
    k, n = w.shape
    w = f64(bf(w)).reshape(k // 32, 32, n)
    amax = np.abs(w).max(1)
    if fmt == "e4m3":
        byte = np.frexp(amax)[1] - 1 + 127 - 7
    else:
        mant, ex = np.frexp(amax / 6.0)
        byte = np.where(mant > 0.5, ex, ex - 1) + 127
    byte = np.clip(np.where(amax > 0, byte, 1), 1, 254)
    scaled = (w * np.exp2(127.0 - byte)[:, None, :]).reshape(k, n).astype(np.float32)
    by_word = np.ascontiguousarray(scaled.reshape(k // 512, 128, 4, n).transpose(0, 1, 3, 2))
    if fmt == "e4m3":
        words = by_word.astype(ml_dtypes.float8_e4m3fn).view(np.uint8)
    else:
        c = by_word.astype(ml_dtypes.float4_e2m1fn).view(np.uint8) & 0xF
        words = c[..., 0::2] | (c[..., 1::2] << 4)
    return np.ascontiguousarray(words), np.ascontiguousarray(byte.astype(np.uint8).reshape(k // 512, 16, n))


def unpack_weight(words, scales, fmt):
    g, p, n, _ = words.shape
    if fmt == "e4m3":
        vals = np.ascontiguousarray(words).view(ml_dtypes.float8_e4m3fn).astype(np.float64)
    else:
        nib = np.empty((g, p, n, 4), np.uint8)
        nib[..., 0::2] = words & 0xF
        nib[..., 1::2] = words >> 4
        vals = E2M1[nib]
    vals = vals * np.repeat(np.exp2(scales.astype(np.float64) - 127.0), 8, axis=1)[..., None]
    return vals.transpose(0, 1, 3, 2).reshape(g * 512, n)

def pack4(w):
    words, scales = pack_weight(w, "e2m1")
    return words.reshape(words.shape[0], 128, -1), scales


def unpack4(words, scales):
    return unpack_weight(words.reshape(words.shape[0], 128, -1, 2), scales, "e2m1")


B, D, H, F, K = 2048, 1024, 1024, 1024, 128
EPS_LN = 1e-5


def silu(v):
    return v / (1.0 + np.exp(-v))


def setup_inputs():
    s = mx_kscale(D)
    x = bf(np.random.standard_normal((B, D)) * s)
    W1_words, W1_scales = pack4(np.random.standard_normal((D, H)) / np.sqrt(D) / s[:, None])
    return {"x": x,
            "W1_words": W1_words,
            "W1_scales": W1_scales,
            "b1": bf(0.2 * np.random.standard_normal(H)),
            "g": bf(1.0 + 0.1 * np.random.standard_normal(H)),
            "beta": bf(0.1 * np.random.standard_normal(H))}


def reference(x, W1_words, W1_scales, b1, g, beta):
    h = silu((mxq(f64(x), 1, "e4m3") @ unpack4(W1_words, W1_scales)) + f64(b1))
    mu = h.mean(-1, keepdims=True)
    var = ((h - mu) ** 2).mean(-1, keepdims=True)
    return (h - mu) / np.sqrt(var + EPS_LN) * f64(g) + f64(beta)

@@ -1,0 +1,173 @@
+from contextlib import ExitStack
+
+import concourse.mybir as mybir
+from concourse.masks import make_identity
+
+F32 = mybir.dt.float32
+BF16 = mybir.dt.bfloat16
+I32 = mybir.dt.int32
+U32 = mybir.dt.uint32
+U8 = mybir.dt.uint8
+FP8X4 = mybir.dt.float8_e4m3fn_x4
+FP4X4 = mybir.dt.float4_e2m1fn_x4
+ACT = mybir.ActivationFunctionType
+ALU = mybir.AluOpType
+
+P = 128
+B, D, H = 2048, 1024, 1024
+EPS_LN = 1e-5
+PACK = 4
+K_PASS = P * PACK
+PASSES = D // K_PASS
+ROW_TILES = B // P
+BANK = 512
+HALVES = H // BANK
+WORDS = K_PASS // 2
+
+FLOPS = 2 * B * D * H
+
+
+def tile_evidentialhead_pa_kernel(tc, x, W1_words, W1_scales, b1, g, beta, out):
+    nc = tc.nc
+    x_rows = x.rearrange("(p t) d -> p t d", t=ROW_TILES)
+    out_rows = out.rearrange("(p t) n -> p t n", t=ROW_TILES)
+
+    with ExitStack() as ctx:
+        const = ctx.enter_context(tc.tile_pool(name="const", bufs=1))
+        x_pool = ctx.enter_context(tc.tile_pool(name="x_pool", bufs=1))
+        quant = ctx.enter_context(tc.tile_pool(name="quant", bufs=3))
+        work = ctx.enter_context(tc.tile_pool(name="work", bufs=4))
+        stats = ctx.enter_context(tc.tile_pool(name="stats", bufs=4))
+        psum_t = ctx.enter_context(tc.psum_pool(name="psum_t", bufs=2))
+        psum_acc = ctx.enter_context(tc.psum_pool(name="psum_acc", bufs=6))
+
+        w_scales = const.tile([P, PASSES, H], U8, align_bytes=64)
+        nc.vector.memset(w_scales[:].bitcast(I32), 0)
+
+        x_sb = [x_pool.tile([P, D], BF16, name="x_sb%d" % t) for t in range(ROW_TILES)]
+        nc.sync.dma_start(out=x_sb[0][:], in_=x_rows[:, 0, :])
+
+        scale_rows = W1_scales.bitcast(I32).rearrange("g (Q r) n -> r Q g n", r=4)
+        for r in range(4):
+            nc.sync.dma_start(out=w_scales[r:P:32, :, :].bitcast(I32), in_=scale_rows[r])
+
+        w_words = const.tile([P, PASSES, 2 * H], U8, align_bytes=64)
+        for gi in range(PASSES):
+            nc.sync.dma_start(out=w_words[:, gi, :].bitcast(I32), in_=W1_words[gi].bitcast(I32))
+
+        for t in range(1, ROW_TILES):
+            nc.sync.dma_start(out=x_sb[t][:], in_=x_rows[:, t, :])
+
+        b1_all = const.tile([P, H], BF16)
+        g_all = const.tile([P, H], BF16)
+        beta_all = const.tile([P, H], BF16)
+        nc.scalar.dma_start(out=b1_all[:], in_=b1.partition_broadcast(P))
+        nc.scalar.dma_start(out=g_all[:], in_=g.partition_broadcast(P))
+        nc.scalar.dma_start(out=beta_all[:], in_=beta.partition_broadcast(P))
+
+        ident = const.tile([P, P], F32)
+        make_identity(nc, ident[:])
+        neg_half = const.tile([P, 1], F32)
+        nc.gpsimd.memset(neg_half[:], -0.5)
+        warm = const.tile([P, 1], F32)
+        nc.gpsimd.memset(warm[:], 0.0)
+        nc.scalar.activation(out=warm[:], in_=warm[:], func=ACT.Silu)
+
+        xt, grouped, codes, x_scales, acc = {}, {}, {}, {}, {}
+        h, centred, neg_mean, rstd = {}, {}, {}, {}
+
+        def transpose_x(t):
+            x_words = x_sb[t][:].bitcast(F32)
+            xt[t] = psum_t.tile([P, PASSES * 2, P], F32, name="xt", tag="xt")
+            for gi in range(PASSES):
+                for u in range(2):
+                    nc.tensor.transpose(
+                        xt[t][:, 2 * gi + u, :],
+                        x_words[:, WORDS * gi + u : WORDS * (gi + 1) : 2],
+                        ident[:],
+                    )
+
+        def group_x(t):
+            grouped[t] = quant.tile([P, PASSES, P, PACK], BF16, name="grouped", tag="grouped", align_bytes=64)
+            nc.scalar.copy(
+                out=grouped[t][:].bitcast(F32),
+                in_=xt[t][:].rearrange("p (g u) r -> p g r u", u=2),
+            )
+
+        def quantise_x(t):
+            codes[t] = quant.tile([P, PASSES * P], U32, name="codes", tag="codes", align_bytes=64)
+            x_scales[t] = quant.tile([P, PASSES * P], U8, name="x_scales", tag="x_scales", align_bytes=64)
+            nc.vector.quantize_mx(
+                out=codes[t][:].bitcast(FP8X4),
+                scales=x_scales[t][:],
+                in_=grouped[t][:].rearrange("p g r t -> p (g r t)"),
+            )
+
+        def multiply(t):
+            for half in range(HALVES):
+                acc[t, half] = psum_acc.tile([P, BANK], F32, name="acc", tag="acc")
+                for gi in range(PASSES):
+                    nc.tensor.matmul_mx(
+                        out=acc[t, half][:],
+                        lhsT=codes[t][:, P * gi : P * (gi + 1)].bitcast(FP8X4),
+                        lhsT_scale=x_scales[t][:, P * gi : P * (gi + 1)],
+                        rhs=w_words[:, gi, 2 * BANK * half : 2 * BANK * (half + 1)].bitcast(FP4X4),
+                        rhs_scale=w_scales[:, gi, BANK * half : BANK * (half + 1)],
+                        start=(gi == 0),
+                        stop=(gi == PASSES - 1),
+                    )
+
+        def add_bias(t):
+            h[t] = work.tile([P, H], F32, name="h", tag="h")
+            for half in range(HALVES):
+                cols = slice(BANK * half, BANK * (half + 1))
+                nc.vector.tensor_tensor(out=h[t][:, cols], in0=acc[t, half][:], in1=b1_all[:, cols], op=ALU.add)
+
+        def silu_and_mean(t):
+            row_sum = stats.tile([P, 1], F32, name="row_sum", tag="row_sum")
+            nc.scalar.activation(out=h[t][:], in_=h[t][:], func=ACT.Silu, accum_out=row_sum[:])
+            neg_mean[t] = stats.tile([P, 1], F32, name="neg_mean", tag="neg_mean")
+            nc.gpsimd.tensor_scalar(
+                out=neg_mean[t][:], in0=row_sum[:], scalar1=-1.0 / H, scalar2=0.0, op0=ALU.mult, op1=ALU.add
+            )
+
+        def variance(t):
+            squares = work.tile([P, H], F32, name="squares", tag="squares")
+            sq_sum = stats.tile([P, 1], F32, name="sq_sum", tag="sq_sum")
+            nc.scalar.activation(
+                out=squares[:], in_=h[t][:], func=ACT.Square, bias=neg_mean[t][:], scale=1.0, accum_out=sq_sum[:]
+            )
+            var_eps = stats.tile([P, 1], F32, name="var_eps", tag="var_eps")
+            nc.gpsimd.tensor_scalar(
+                out=var_eps[:], in0=sq_sum[:], scalar1=1.0 / H, scalar2=EPS_LN, op0=ALU.mult, op1=ALU.add
+            )
+            rstd[t] = stats.tile([P, 1], F32, name="rstd", tag="rstd")
+            nc.gpsimd.tensor_tensor(out=rstd[t][:], in0=var_eps[:], in1=neg_half[:], op=ALU.pow)
+
+        def centre_and_gain(t):
+            centred[t] = work.tile([P, H], F32, name="centred", tag="centred")
+            nc.vector.scalar_tensor_tensor(
+                out=centred[t][:], in0=h[t][:], scalar=neg_mean[t][:], in1=g_all[:], op0=ALU.add, op1=ALU.mult
+            )
+
+        def scale_shift_store(t):
+            result = work.tile([P, H], F32, name="result", tag="result")
+            nc.vector.scalar_tensor_tensor(
+                out=result[:], in0=centred[t][:], scalar=rstd[t][:], in1=beta_all[:], op0=ALU.mult, op1=ALU.add
+            )
+            nc.sync.dma_start(out=out_rows[:, t, :], in_=result[:])
+
+        def run(stage, t):
+            if 0 <= t < ROW_TILES:
+                stage(t)
+
+        for i in range(-3, ROW_TILES + 1):
+            run(multiply, i + 2)
+            run(transpose_x, i + 3)
+            run(add_bias, i + 1)
+            run(variance, i)
+            run(centre_and_gain, i)
+            run(group_x, i + 3)
+            run(scale_shift_store, i - 1)
+            run(silu_and_mean, i + 1)
+            run(quantise_x, i + 3)

@@ -40,6 +40,7 @@ def tile_evidentialhead_pa_kernel(tc, x, W1_words, W1_scales, b1, g, beta, out):
         stats = ctx.enter_context(tc.tile_pool(name="stats", bufs=4))
         psum_t = ctx.enter_context(tc.psum_pool(name="psum_t", bufs=2))
         psum_acc = ctx.enter_context(tc.psum_pool(name="psum_acc", bufs=6))
+        ctx.enter_context(tc.manual_schedule())
 
         w_scales = const.tile([P, PASSES, H], U8, align_bytes=64)
         nc.vector.memset(w_scales[:].bitcast(I32), 0)

@@ -162,13 +162,13 @@ def tile_evidentialhead_pa_kernel(tc, x, W1_words, W1_scales, b1, g, beta, out):
             if 0 <= t < ROW_TILES:
                 stage(t)
 
-        for i in range(-3, ROW_TILES + 1):
-            run(multiply, i + 2)
-            run(transpose_x, i + 3)
-            run(add_bias, i + 1)
-            run(variance, i)
-            run(centre_and_gain, i)
-            run(group_x, i + 3)
-            run(scale_shift_store, i - 1)
-            run(silu_and_mean, i + 1)
-            run(quantise_x, i + 3)
+        for j in range(ROW_TILES + 7):
+            run(multiply, j - 3)
+            run(transpose_x, j)
+            run(add_bias, j - 4)
+            run(silu_and_mean, j - 5)
+            run(variance, j - 6)
+            run(centre_and_gain, j - 6)
+            run(group_x, j - 1)
+            run(scale_shift_store, j - 7)
+            run(quantise_x, j - 2)

@@ -23,6 +23,8 @@ ROW_TILES = B // P
 BANK = 512
 HALVES = H // BANK
 WORDS = K_PASS // 2
+V_COLS = 512
+GAIN_LAG = 6
 
 FLOPS = 2 * B * D * H
 
@@ -39,7 +41,8 @@ def tile_evidentialhead_pa_kernel(tc, x, W1_words, W1_scales, b1, g, beta, out):
         work = ctx.enter_context(tc.tile_pool(name="work", bufs=4))
         stats = ctx.enter_context(tc.tile_pool(name="stats", bufs=4))
         psum_t = ctx.enter_context(tc.psum_pool(name="psum_t", bufs=2))
-        psum_acc = ctx.enter_context(tc.psum_pool(name="psum_acc", bufs=6))
+        psum_acc = ctx.enter_context(tc.psum_pool(name="psum_acc", bufs=4))
+        psum_const = ctx.enter_context(tc.psum_pool(name="psum_const", bufs=1))
         ctx.enter_context(tc.manual_schedule())
 
         w_scales = const.tile([P, PASSES, H], U8, align_bytes=64)
@@ -68,6 +71,8 @@ def tile_evidentialhead_pa_kernel(tc, x, W1_words, W1_scales, b1, g, beta, out):
 
         ident = const.tile([P, P], F32)
         make_identity(nc, ident[:])
+        ident_bf = const.tile([P, P], BF16)
+        make_identity(nc, ident_bf[:])
         neg_half = const.tile([P, 1], F32)
         nc.gpsimd.memset(neg_half[:], -0.5)
         warm = const.tile([P, 1], F32)
@@ -76,6 +81,15 @@ def tile_evidentialhead_pa_kernel(tc, x, W1_words, W1_scales, b1, g, beta, out):
 
         xt, grouped, codes, x_scales, acc = {}, {}, {}, {}, {}
         h, centred, neg_mean, rstd = {}, {}, {}, {}
+
+        g_ps = psum_const.tile([P, H], BF16)
+        beta_ps = psum_const.tile([P, H], BF16)
+
+        def copy_gain_and_shift_to_psum():
+            for dst, src in ((g_ps, g_all), (beta_ps, beta_all)):
+                for half in range(HALVES):
+                    cols = slice(BANK * half, BANK * (half + 1))
+                    nc.tensor.matmul(out=dst[:, cols], lhsT=ident_bf[:], rhs=src[:, cols], start=True, stop=True)
 
         def transpose_x(t):
             x_words = x_sb[t][:].bitcast(F32)
@@ -148,13 +162,29 @@ def tile_evidentialhead_pa_kernel(tc, x, W1_words, W1_scales, b1, g, beta, out):
         def centre_and_gain(t):
             centred[t] = work.tile([P, H], F32, name="centred", tag="centred")
             nc.vector.scalar_tensor_tensor(
-                out=centred[t][:], in0=h[t][:], scalar=neg_mean[t][:], in1=g_all[:], op0=ALU.add, op1=ALU.mult
+                out=centred[t][:], in0=h[t][:], scalar=neg_mean[t][:], in1=g_ps[:], op0=ALU.add, op1=ALU.mult
             )
 
         def scale_shift_store(t):
             result = work.tile([P, H], F32, name="result", tag="result")
             nc.vector.scalar_tensor_tensor(
-                out=result[:], in0=centred[t][:], scalar=rstd[t][:], in1=beta_all[:], op0=ALU.mult, op1=ALU.add
+                out=result[:, :V_COLS],
+                in0=centred[t][:, :V_COLS],
+                scalar=rstd[t][:],
+                in1=beta_ps[:, :V_COLS],
+                op0=ALU.mult,
+                op1=ALU.add,
+            )
+            nc.gpsimd.tensor_scalar(
+                out=centred[t][:, V_COLS:],
+                in0=centred[t][:, V_COLS:],
+                scalar1=rstd[t][:],
+                scalar2=0.0,
+                op0=ALU.mult,
+                op1=ALU.add,
+            )
+            nc.gpsimd.tensor_tensor(
+                out=result[:, V_COLS:], in0=centred[t][:, V_COLS:], in1=beta_all[:, V_COLS:], op=ALU.add
             )
             nc.sync.dma_start(out=out_rows[:, t, :], in_=result[:])
 
@@ -165,10 +195,12 @@ def tile_evidentialhead_pa_kernel(tc, x, W1_words, W1_scales, b1, g, beta, out):
         for j in range(ROW_TILES + 7):
             run(multiply, j - 3)
             run(transpose_x, j)
+            if j == GAIN_LAG - 1:
+                copy_gain_and_shift_to_psum()
+            run(scale_shift_store, j - 7)
             run(add_bias, j - 4)
             run(silu_and_mean, j - 5)
-            run(variance, j - 6)
-            run(centre_and_gain, j - 6)
+            run(variance, j - GAIN_LAG)
+            run(centre_and_gain, j - GAIN_LAG)
             run(group_x, j - 1)
-            run(scale_shift_store, j - 7)
             run(quantise_x, j - 2)

@@ -23,8 +23,14 @@ ROW_TILES = B // P
 BANK = 512
 HALVES = H // BANK
 WORDS = K_PASS // 2
-V_COLS = 512
-GAIN_LAG = 6
+
+GROUP_LAG = 1
+QUANTISE_LAG = 2
+MULTIPLY_LAG = 3
+BIAS_LAG = 4
+SILU_LAG = 5
+CENTRE_LAG = 6
+STORE_LAG = 8
 
 FLOPS = 2 * B * D * H
 
@@ -41,8 +47,7 @@ def tile_evidentialhead_pa_kernel(tc, x, W1_words, W1_scales, b1, g, beta, out):
         work = ctx.enter_context(tc.tile_pool(name="work", bufs=4))
         stats = ctx.enter_context(tc.tile_pool(name="stats", bufs=4))
         psum_t = ctx.enter_context(tc.psum_pool(name="psum_t", bufs=2))
-        psum_acc = ctx.enter_context(tc.psum_pool(name="psum_acc", bufs=4))
-        psum_const = ctx.enter_context(tc.psum_pool(name="psum_const", bufs=1))
+        psum_acc = ctx.enter_context(tc.psum_pool(name="psum_acc", bufs=6))
         ctx.enter_context(tc.manual_schedule())
 
         w_scales = const.tile([P, PASSES, H], U8, align_bytes=64)
@@ -59,20 +64,18 @@ def tile_evidentialhead_pa_kernel(tc, x, W1_words, W1_scales, b1, g, beta, out):
         for gi in range(PASSES):
             nc.sync.dma_start(out=w_words[:, gi, :].bitcast(I32), in_=W1_words[gi].bitcast(I32))
 
-        for t in range(1, ROW_TILES):
-            nc.sync.dma_start(out=x_sb[t][:], in_=x_rows[:, t, :])
-
         b1_all = const.tile([P, H], BF16)
         g_all = const.tile([P, H], BF16)
         beta_all = const.tile([P, H], BF16)
         nc.scalar.dma_start(out=b1_all[:], in_=b1.partition_broadcast(P))
-        nc.scalar.dma_start(out=g_all[:], in_=g.partition_broadcast(P))
-        nc.scalar.dma_start(out=beta_all[:], in_=beta.partition_broadcast(P))
+        for t in range(1, ROW_TILES):
+            nc.sync.dma_start(out=x_sb[t][:], in_=x_rows[:, t, :])
+            if t == MULTIPLY_LAG:
+                nc.sync.dma_start(out=g_all[:], in_=g.partition_broadcast(P))
+                nc.sync.dma_start(out=beta_all[:], in_=beta.partition_broadcast(P))
 
         ident = const.tile([P, P], F32)
         make_identity(nc, ident[:])
-        ident_bf = const.tile([P, P], BF16)
-        make_identity(nc, ident_bf[:])
         neg_half = const.tile([P, 1], F32)
         nc.gpsimd.memset(neg_half[:], -0.5)
         warm = const.tile([P, 1], F32)
@@ -81,15 +84,6 @@ def tile_evidentialhead_pa_kernel(tc, x, W1_words, W1_scales, b1, g, beta, out):
 
         xt, grouped, codes, x_scales, acc = {}, {}, {}, {}, {}
         h, centred, neg_mean, rstd = {}, {}, {}, {}
-
-        g_ps = psum_const.tile([P, H], BF16)
-        beta_ps = psum_const.tile([P, H], BF16)
-
-        def copy_gain_and_shift_to_psum():
-            for dst, src in ((g_ps, g_all), (beta_ps, beta_all)):
-                for half in range(HALVES):
-                    cols = slice(BANK * half, BANK * (half + 1))
-                    nc.tensor.matmul(out=dst[:, cols], lhsT=ident_bf[:], rhs=src[:, cols], start=True, stop=True)
 
         def transpose_x(t):
             x_words = x_sb[t][:].bitcast(F32)
@@ -162,45 +156,36 @@ def tile_evidentialhead_pa_kernel(tc, x, W1_words, W1_scales, b1, g, beta, out):
         def centre_and_gain(t):
             centred[t] = work.tile([P, H], F32, name="centred", tag="centred")
             nc.vector.scalar_tensor_tensor(
-                out=centred[t][:], in0=h[t][:], scalar=neg_mean[t][:], in1=g_ps[:], op0=ALU.add, op1=ALU.mult
+                out=centred[t][:], in0=h[t][:], scalar=neg_mean[t][:], in1=g_all[:], op0=ALU.add, op1=ALU.mult
             )
 
         def scale_shift_store(t):
+            pieces = 2 if t == ROW_TILES - 1 else 1
+            width = H // pieces
             result = work.tile([P, H], F32, name="result", tag="result")
-            nc.vector.scalar_tensor_tensor(
-                out=result[:, :V_COLS],
-                in0=centred[t][:, :V_COLS],
-                scalar=rstd[t][:],
-                in1=beta_ps[:, :V_COLS],
-                op0=ALU.mult,
-                op1=ALU.add,
-            )
-            nc.gpsimd.tensor_scalar(
-                out=centred[t][:, V_COLS:],
-                in0=centred[t][:, V_COLS:],
-                scalar1=rstd[t][:],
-                scalar2=0.0,
-                op0=ALU.mult,
-                op1=ALU.add,
-            )
-            nc.gpsimd.tensor_tensor(
-                out=result[:, V_COLS:], in0=centred[t][:, V_COLS:], in1=beta_all[:, V_COLS:], op=ALU.add
-            )
-            nc.sync.dma_start(out=out_rows[:, t, :], in_=result[:])
+            for piece in range(pieces):
+                cols = slice(width * piece, width * (piece + 1))
+                nc.vector.scalar_tensor_tensor(
+                    out=result[:, cols],
+                    in0=centred[t][:, cols],
+                    scalar=rstd[t][:],
+                    in1=beta_all[:, cols],
+                    op0=ALU.mult,
+                    op1=ALU.add,
+                )
+                nc.sync.dma_start(out=out_rows[:, t, cols], in_=result[:, cols])
 
         def run(stage, t):
             if 0 <= t < ROW_TILES:
                 stage(t)
 
-        for j in range(ROW_TILES + 7):
-            run(multiply, j - 3)
+        for j in range(ROW_TILES + STORE_LAG):
+            run(multiply, j - MULTIPLY_LAG)
             run(transpose_x, j)
-            if j == GAIN_LAG - 1:
-                copy_gain_and_shift_to_psum()
-            run(scale_shift_store, j - 7)
-            run(add_bias, j - 4)
-            run(silu_and_mean, j - 5)
-            run(variance, j - GAIN_LAG)
-            run(centre_and_gain, j - GAIN_LAG)
-            run(group_x, j - 1)
-            run(quantise_x, j - 2)
+            run(add_bias, j - BIAS_LAG)
+            run(silu_and_mean, j - SILU_LAG)
+            run(variance, j - CENTRE_LAG)
+            run(centre_and_gain, j - CENTRE_LAG)
+            run(group_x, j - GROUP_LAG)
+            run(scale_shift_store, j - STORE_LAG)
+            run(quantise_x, j - QUANTISE_LAG)

@@ -47,7 +47,8 @@ def tile_evidentialhead_pa_kernel(tc, x, W1_words, W1_scales, b1, g, beta, out):
         work = ctx.enter_context(tc.tile_pool(name="work", bufs=4))
         stats = ctx.enter_context(tc.tile_pool(name="stats", bufs=4))
         psum_t = ctx.enter_context(tc.psum_pool(name="psum_t", bufs=2))
-        psum_acc = ctx.enter_context(tc.psum_pool(name="psum_acc", bufs=6))
+        psum_acc = ctx.enter_context(tc.psum_pool(name="psum_acc", bufs=4))
+        psum_vec = ctx.enter_context(tc.psum_pool(name="psum_vec", bufs=1))
         ctx.enter_context(tc.manual_schedule())
 
         w_scales = const.tile([P, PASSES, H], U8, align_bytes=64)
@@ -65,14 +66,17 @@ def tile_evidentialhead_pa_kernel(tc, x, W1_words, W1_scales, b1, g, beta, out):
             nc.sync.dma_start(out=w_words[:, gi, :].bitcast(I32), in_=W1_words[gi].bitcast(I32))
 
         b1_all = const.tile([P, H], BF16)
-        g_all = const.tile([P, H], BF16)
-        beta_all = const.tile([P, H], BF16)
         nc.scalar.dma_start(out=b1_all[:], in_=b1.partition_broadcast(P))
+        vec_rows = const.tile([P, 2, H], BF16)
+        nc.vector.memset(vec_rows[:], 0.0)
+        ones = const.tile([P, P], BF16)
+        nc.vector.memset(ones[:], 1.0)
+        nc.scalar.dma_start(out=vec_rows[0:1, 0, :], in_=g.rearrange("(o n) -> o n", o=1))
+        nc.scalar.dma_start(out=vec_rows[0:1, 1, :], in_=beta.rearrange("(o n) -> o n", o=1))
+        g_all = psum_vec.tile([P, H], BF16, name="g_all")
+        beta_all = psum_vec.tile([P, H], BF16, name="beta_all")
         for t in range(1, ROW_TILES):
             nc.sync.dma_start(out=x_sb[t][:], in_=x_rows[:, t, :])
-            if t == MULTIPLY_LAG:
-                nc.sync.dma_start(out=g_all[:], in_=g.partition_broadcast(P))
-                nc.sync.dma_start(out=beta_all[:], in_=beta.partition_broadcast(P))
 
         ident = const.tile([P, P], F32)
         make_identity(nc, ident[:])
@@ -175,6 +179,14 @@ def tile_evidentialhead_pa_kernel(tc, x, W1_words, W1_scales, b1, g, beta, out):
                 )
                 nc.sync.dma_start(out=out_rows[:, t, cols], in_=result[:, cols])
 
+        def spread_vectors():
+            for which, spread in enumerate((g_all, beta_all)):
+                for half in range(HALVES):
+                    cols = slice(BANK * half, BANK * (half + 1))
+                    nc.tensor.matmul(
+                        spread[:, cols], lhsT=ones[:], rhs=vec_rows[:, which, cols], start=True, stop=True
+                    )
+
         def run(stage, t):
             if 0 <= t < ROW_TILES:
                 stage(t)
@@ -182,6 +194,8 @@ def tile_evidentialhead_pa_kernel(tc, x, W1_words, W1_scales, b1, g, beta, out):
         for j in range(ROW_TILES + STORE_LAG):
             run(multiply, j - MULTIPLY_LAG)
             run(transpose_x, j)
+            if j == GROUP_LAG:
+                spread_vectors()
             run(add_bias, j - BIAS_LAG)
             run(silu_and_mean, j - SILU_LAG)
             run(variance, j - CENTRE_LAG)

@@ -51,8 +51,20 @@ def tile_evidentialhead_pa_kernel(tc, x, W1_words, W1_scales, b1, g, beta, out):
         psum_vec = ctx.enter_context(tc.psum_pool(name="psum_vec", bufs=1))
         ctx.enter_context(tc.manual_schedule())
 
+        warm = const.tile([P, 1], F32)
+        nc.gpsimd.memset(warm[:], 0.0)
+        nc.scalar.activation(out=warm[:], in_=warm[:], func=ACT.Silu)
+        ident = const.tile([P, P], F32)
+        make_identity(nc, ident[:])
+        neg_half = const.tile([P, 1], F32)
+        nc.gpsimd.memset(neg_half[:], -0.5)
+
         w_scales = const.tile([P, PASSES, H], U8, align_bytes=64)
         nc.vector.memset(w_scales[:].bitcast(I32), 0)
+        vec_rows = const.tile([P, 3, H], BF16)
+        nc.vector.memset(vec_rows[:], 0.0)
+        ones = const.tile([P, P], BF16)
+        nc.vector.memset(ones[:], 1.0)
 
         x_sb = [x_pool.tile([P, D], BF16, name="x_sb%d" % t) for t in range(ROW_TILES)]
         nc.sync.dma_start(out=x_sb[0][:], in_=x_rows[:, 0, :])
@@ -65,26 +77,14 @@ def tile_evidentialhead_pa_kernel(tc, x, W1_words, W1_scales, b1, g, beta, out):
         for gi in range(PASSES):
             nc.sync.dma_start(out=w_words[:, gi, :].bitcast(I32), in_=W1_words[gi].bitcast(I32))
 
-        b1_all = const.tile([P, H], BF16)
-        nc.scalar.dma_start(out=b1_all[:], in_=b1.partition_broadcast(P))
-        vec_rows = const.tile([P, 2, H], BF16)
-        nc.vector.memset(vec_rows[:], 0.0)
-        ones = const.tile([P, P], BF16)
-        nc.vector.memset(ones[:], 1.0)
-        nc.scalar.dma_start(out=vec_rows[0:1, 0, :], in_=g.rearrange("(o n) -> o n", o=1))
-        nc.scalar.dma_start(out=vec_rows[0:1, 1, :], in_=beta.rearrange("(o n) -> o n", o=1))
-        g_all = psum_vec.tile([P, H], BF16, name="g_all")
-        beta_all = psum_vec.tile([P, H], BF16, name="beta_all")
+        for which, vec in enumerate((b1, g, beta)):
+            nc.sync.dma_start(out=vec_rows[0:1, which, :], in_=vec.rearrange("(o n) -> o n", o=1))
         for t in range(1, ROW_TILES):
             nc.sync.dma_start(out=x_sb[t][:], in_=x_rows[:, t, :])
 
-        ident = const.tile([P, P], F32)
-        make_identity(nc, ident[:])
-        neg_half = const.tile([P, 1], F32)
-        nc.gpsimd.memset(neg_half[:], -0.5)
-        warm = const.tile([P, 1], F32)
-        nc.gpsimd.memset(warm[:], 0.0)
-        nc.scalar.activation(out=warm[:], in_=warm[:], func=ACT.Silu)
+        b1_all = const.tile([P, H], BF16)
+        g_all = psum_vec.tile([P, H], BF16, name="g_all")
+        beta_all = psum_vec.tile([P, H], BF16, name="beta_all")
 
         xt, grouped, codes, x_scales, acc = {}, {}, {}, {}, {}
         h, centred, neg_mean, rstd = {}, {}, {}, {}
@@ -180,12 +180,14 @@ def tile_evidentialhead_pa_kernel(tc, x, W1_words, W1_scales, b1, g, beta, out):
                 nc.sync.dma_start(out=out_rows[:, t, cols], in_=result[:, cols])
 
         def spread_vectors():
-            for which, spread in enumerate((g_all, beta_all)):
+            b1_ps = psum_acc.tile([P, H], BF16, name="b1_ps", tag="acc")
+            for which, spread in enumerate((b1_ps, g_all, beta_all)):
                 for half in range(HALVES):
                     cols = slice(BANK * half, BANK * (half + 1))
                     nc.tensor.matmul(
                         spread[:, cols], lhsT=ones[:], rhs=vec_rows[:, which, cols], start=True, stop=True
                     )
+            nc.scalar.copy(out=b1_all[:], in_=b1_ps[:])
 
         def run(stage, t):
             if 0 <= t < ROW_TILES:
@@ -194,12 +196,12 @@ def tile_evidentialhead_pa_kernel(tc, x, W1_words, W1_scales, b1, g, beta, out):
         for j in range(ROW_TILES + STORE_LAG):
             run(multiply, j - MULTIPLY_LAG)
             run(transpose_x, j)
-            if j == GROUP_LAG:
-                spread_vectors()
             run(add_bias, j - BIAS_LAG)
             run(silu_and_mean, j - SILU_LAG)
             run(variance, j - CENTRE_LAG)
             run(centre_and_gain, j - CENTRE_LAG)
             run(group_x, j - GROUP_LAG)
+            if j == GROUP_LAG:
+                spread_vectors()
             run(scale_shift_store, j - STORE_LAG)
             run(quantise_x, j - QUANTISE_LAG)

@@ -59,28 +59,33 @@ def tile_evidentialhead_pa_kernel(tc, x, W1_words, W1_scales, b1, g, beta, out):
         neg_half = const.tile([P, 1], F32)
         nc.gpsimd.memset(neg_half[:], -0.5)
 
+        b1_row = const.tile([P, H], BF16)
+        nc.vector.memset(b1_row[:], 0.0)
         w_scales = const.tile([P, PASSES, H], U8, align_bytes=64)
         nc.vector.memset(w_scales[:].bitcast(I32), 0)
-        vec_rows = const.tile([P, 3, H], BF16)
-        nc.vector.memset(vec_rows[:], 0.0)
         ones = const.tile([P, P], BF16)
         nc.vector.memset(ones[:], 1.0)
+        norm_rows = const.tile([P, 2, H], BF16)
+        nc.vector.memset(norm_rows[:], 0.0)
 
         x_sb = [x_pool.tile([P, D], BF16, name="x_sb%d" % t) for t in range(ROW_TILES)]
         nc.sync.dma_start(out=x_sb[0][:], in_=x_rows[:, 0, :])
+
+        w_words = const.tile([P, PASSES, 2 * H], U8, align_bytes=64)
+        nc.sync.dma_start(
+            out=w_words[:].bitcast(I32), in_=W1_words.bitcast(I32).rearrange("g p n -> p g n")
+        )
+        nc.sync.dma_start(out=b1_row[0:1, :], in_=b1.rearrange("(o n) -> o n", o=1))
 
         scale_rows = W1_scales.bitcast(I32).rearrange("g (Q r) n -> r Q g n", r=4)
         for r in range(4):
             nc.sync.dma_start(out=w_scales[r:P:32, :, :].bitcast(I32), in_=scale_rows[r])
 
-        w_words = const.tile([P, PASSES, 2 * H], U8, align_bytes=64)
-        for gi in range(PASSES):
-            nc.sync.dma_start(out=w_words[:, gi, :].bitcast(I32), in_=W1_words[gi].bitcast(I32))
-
-        for which, vec in enumerate((b1, g, beta)):
-            nc.sync.dma_start(out=vec_rows[0:1, which, :], in_=vec.rearrange("(o n) -> o n", o=1))
         for t in range(1, ROW_TILES):
             nc.sync.dma_start(out=x_sb[t][:], in_=x_rows[:, t, :])
+            if t == MULTIPLY_LAG:
+                for which, vec in enumerate((g, beta)):
+                    nc.sync.dma_start(out=norm_rows[0:1, which, :], in_=vec.rearrange("(o n) -> o n", o=1))
 
         b1_all = const.tile([P, H], BF16)
         g_all = psum_vec.tile([P, H], BF16, name="g_all")
@@ -179,15 +184,19 @@ def tile_evidentialhead_pa_kernel(tc, x, W1_words, W1_scales, b1, g, beta, out):
                 )
                 nc.sync.dma_start(out=out_rows[:, t, cols], in_=result[:, cols])
 
-        def spread_vectors():
+        def spread(row, target):
+            for half in range(HALVES):
+                cols = slice(BANK * half, BANK * (half + 1))
+                nc.tensor.matmul(target[:, cols], lhsT=ones[:], rhs=row[:, cols], start=True, stop=True)
+
+        def spread_b1():
             b1_ps = psum_acc.tile([P, H], BF16, name="b1_ps", tag="acc")
-            for which, spread in enumerate((b1_ps, g_all, beta_all)):
-                for half in range(HALVES):
-                    cols = slice(BANK * half, BANK * (half + 1))
-                    nc.tensor.matmul(
-                        spread[:, cols], lhsT=ones[:], rhs=vec_rows[:, which, cols], start=True, stop=True
-                    )
+            spread(b1_row, b1_ps)
             nc.scalar.copy(out=b1_all[:], in_=b1_ps[:])
+
+        def spread_g_beta():
+            spread(norm_rows[:, 0, :], g_all)
+            spread(norm_rows[:, 1, :], beta_all)
 
         def run(stage, t):
             if 0 <= t < ROW_TILES:
@@ -201,7 +210,9 @@ def tile_evidentialhead_pa_kernel(tc, x, W1_words, W1_scales, b1, g, beta, out):
             run(variance, j - CENTRE_LAG)
             run(centre_and_gain, j - CENTRE_LAG)
             run(group_x, j - GROUP_LAG)
-            if j == GROUP_LAG:
-                spread_vectors()
+            if j == QUANTISE_LAG:
+                spread_b1()
+            if j == SILU_LAG:
+                spread_g_beta()
             run(scale_shift_store, j - STORE_LAG)
             run(quantise_x, j - QUANTISE_LAG)

@@ -92,7 +92,7 @@ def tile_evidentialhead_pa_kernel(tc, x, W1_words, W1_scales, b1, g, beta, out):
         beta_all = psum_vec.tile([P, H], BF16, name="beta_all")
 
         xt, grouped, codes, x_scales, acc = {}, {}, {}, {}, {}
-        h, centred, neg_mean, rstd = {}, {}, {}, {}
+        h, centred, neg_mean, rstd, row_sums, sq_sums = {}, {}, {}, {}, {}, {}
 
         def transpose_x(t):
             x_words = x_sb[t][:].bitcast(F32)
@@ -144,10 +144,11 @@ def tile_evidentialhead_pa_kernel(tc, x, W1_words, W1_scales, b1, g, beta, out):
         def silu_and_mean(t):
             row_sum = stats.tile([P, 1], F32, name="row_sum", tag="row_sum")
             nc.scalar.activation(out=h[t][:], in_=h[t][:], func=ACT.Silu, accum_out=row_sum[:])
+            row_sums[t] = row_sum
+
+        def mean(t):
             neg_mean[t] = stats.tile([P, 1], F32, name="neg_mean", tag="neg_mean")
-            nc.gpsimd.tensor_scalar(
-                out=neg_mean[t][:], in0=row_sum[:], scalar1=-1.0 / H, scalar2=0.0, op0=ALU.mult, op1=ALU.add
-            )
+            nc.scalar.activation(out=neg_mean[t][:], in_=row_sums[t][:], func=ACT.Copy, scale=-1.0 / H)
 
         def variance(t):
             squares = work.tile([P, H], F32, name="squares", tag="squares")
@@ -155,10 +156,11 @@ def tile_evidentialhead_pa_kernel(tc, x, W1_words, W1_scales, b1, g, beta, out):
             nc.scalar.activation(
                 out=squares[:], in_=h[t][:], func=ACT.Square, bias=neg_mean[t][:], scale=1.0, accum_out=sq_sum[:]
             )
+            sq_sums[t] = sq_sum
+
+        def reciprocal_std(t):
             var_eps = stats.tile([P, 1], F32, name="var_eps", tag="var_eps")
-            nc.gpsimd.tensor_scalar(
-                out=var_eps[:], in0=sq_sum[:], scalar1=1.0 / H, scalar2=EPS_LN, op0=ALU.mult, op1=ALU.add
-            )
+            nc.scalar.activation(out=var_eps[:], in_=sq_sums[t][:], func=ACT.Copy, scale=1.0 / H, bias=EPS_LN)
             rstd[t] = stats.tile([P, 1], F32, name="rstd", tag="rstd")
             nc.gpsimd.tensor_tensor(out=rstd[t][:], in0=var_eps[:], in1=neg_half[:], op=ALU.pow)
 
@@ -208,8 +210,10 @@ def tile_evidentialhead_pa_kernel(tc, x, W1_words, W1_scales, b1, g, beta, out):
             run(add_bias, j - BIAS_LAG)
             run(silu_and_mean, j - SILU_LAG)
             run(variance, j - CENTRE_LAG)
+            run(mean, j - SILU_LAG)
             run(centre_and_gain, j - CENTRE_LAG)
             run(group_x, j - GROUP_LAG)
+            run(reciprocal_std, j - CENTRE_LAG)
             if j == QUANTISE_LAG:
                 spread_b1()
             if j == SILU_LAG:

@@ -29,8 +29,10 @@ QUANTISE_LAG = 2
 MULTIPLY_LAG = 3
 BIAS_LAG = 4
 SILU_LAG = 5
-CENTRE_LAG = 6
+VARIANCE_LAG = 6
+CENTRE_LAG = 7
 STORE_LAG = 8
+POOL_COLS = 256
 
 FLOPS = 2 * B * D * H
 
@@ -90,9 +92,10 @@ def tile_evidentialhead_pa_kernel(tc, x, W1_words, W1_scales, b1, g, beta, out):
         b1_all = const.tile([P, H], BF16)
         g_all = psum_vec.tile([P, H], BF16, name="g_all")
         beta_all = psum_vec.tile([P, H], BF16, name="beta_all")
+        beta_sb = const.tile([P, POOL_COLS], BF16)
 
         xt, grouped, codes, x_scales, acc = {}, {}, {}, {}, {}
-        h, centred, neg_mean, rstd, row_sums, sq_sums = {}, {}, {}, {}, {}, {}
+        h, centred, neg_mean, rstd, row_sums, sq_sums, results = {}, {}, {}, {}, {}, {}, {}
 
         def transpose_x(t):
             x_words = x_sb[t][:].bitcast(F32)
@@ -170,10 +173,32 @@ def tile_evidentialhead_pa_kernel(tc, x, W1_words, W1_scales, b1, g, beta, out):
                 out=centred[t][:], in0=h[t][:], scalar=neg_mean[t][:], in1=g_all[:], op0=ALU.add, op1=ALU.mult
             )
 
+        def gpsimd_share(t):
+            results[t] = work.tile([P, H], F32, name="result", tag="result")
+            if t < ROW_TILES - 1:
+                theirs = slice(H - POOL_COLS, H)
+                scaled = work.tile([P, POOL_COLS], F32, name="scaled", tag="scaled")
+                nc.gpsimd.tensor_scalar(
+                    out=scaled[:], in0=centred[t][:, theirs], scalar1=rstd[t][:], scalar2=0.0, op0=ALU.mult, op1=ALU.add
+                )
+                nc.gpsimd.tensor_tensor(out=results[t][:, theirs], in0=scaled[:], in1=beta_sb[:], op=ALU.add)
+
         def scale_shift_store(t):
-            pieces = 2 if t == ROW_TILES - 1 else 1
+            result = results[t]
+            if t < ROW_TILES - 1:
+                mine = slice(0, H - POOL_COLS)
+                nc.vector.scalar_tensor_tensor(
+                    out=result[:, mine],
+                    in0=centred[t][:, mine],
+                    scalar=rstd[t][:],
+                    in1=beta_all[:, mine],
+                    op0=ALU.mult,
+                    op1=ALU.add,
+                )
+                nc.sync.dma_start(out=out_rows[:, t, :], in_=result[:])
+                return
+            pieces = 2
             width = H // pieces
-            result = work.tile([P, H], F32, name="result", tag="result")
             for piece in range(pieces):
                 cols = slice(width * piece, width * (piece + 1))
                 nc.vector.scalar_tensor_tensor(
@@ -199,6 +224,7 @@ def tile_evidentialhead_pa_kernel(tc, x, W1_words, W1_scales, b1, g, beta, out):
         def spread_g_beta():
             spread(norm_rows[:, 0, :], g_all)
             spread(norm_rows[:, 1, :], beta_all)
+            nc.scalar.copy(out=beta_sb[:], in_=beta_all[:, H - POOL_COLS : H])
 
         def run(stage, t):
             if 0 <= t < ROW_TILES:
@@ -207,16 +233,17 @@ def tile_evidentialhead_pa_kernel(tc, x, W1_words, W1_scales, b1, g, beta, out):
         for j in range(ROW_TILES + STORE_LAG):
             run(multiply, j - MULTIPLY_LAG)
             run(transpose_x, j)
+            run(centre_and_gain, j - CENTRE_LAG)
+            run(gpsimd_share, j - CENTRE_LAG)
             run(add_bias, j - BIAS_LAG)
             run(silu_and_mean, j - SILU_LAG)
-            run(variance, j - CENTRE_LAG)
+            run(variance, j - VARIANCE_LAG)
             run(mean, j - SILU_LAG)
-            run(centre_and_gain, j - CENTRE_LAG)
             run(group_x, j - GROUP_LAG)
-            run(reciprocal_std, j - CENTRE_LAG)
+            run(reciprocal_std, j - VARIANCE_LAG)
             if j == QUANTISE_LAG:
                 spread_b1()
             if j == SILU_LAG:
                 spread_g_beta()
-            run(scale_shift_store, j - STORE_LAG)
             run(quantise_x, j - QUANTISE_LAG)
+            run(scale_shift_store, j - STORE_LAG)

@@ -32,6 +32,7 @@ SILU_LAG = 5
 VARIANCE_LAG = 6
 CENTRE_LAG = 7
 STORE_LAG = 8
+WARM_UP_MATMULS = 10
 POOL_COLS = 256
 
 FLOPS = 2 * B * D * H
@@ -61,14 +62,14 @@ def tile_evidentialhead_pa_kernel(tc, x, W1_words, W1_scales, b1, g, beta, out):
         neg_half = const.tile([P, 1], F32)
         nc.gpsimd.memset(neg_half[:], -0.5)
 
-        b1_row = const.tile([P, H], BF16)
-        nc.vector.memset(b1_row[:], 0.0)
-        w_scales = const.tile([P, PASSES, H], U8, align_bytes=64)
-        nc.vector.memset(w_scales[:].bitcast(I32), 0)
         ones = const.tile([P, P], BF16)
         nc.vector.memset(ones[:], 1.0)
+        b1_row = const.tile([P, H], BF16)
+        nc.vector.memset(b1_row[:].bitcast(I32), 0)
+        w_scales = const.tile([P, PASSES, H], U8, align_bytes=64)
+        nc.vector.memset(w_scales[:].bitcast(I32), 0)
         norm_rows = const.tile([P, 2, H], BF16)
-        nc.vector.memset(norm_rows[:], 0.0)
+        nc.vector.memset(norm_rows[:].bitcast(I32), 0)
 
         x_sb = [x_pool.tile([P, D], BF16, name="x_sb%d" % t) for t in range(ROW_TILES)]
         nc.sync.dma_start(out=x_sb[0][:], in_=x_rows[:, 0, :])
@@ -93,6 +94,10 @@ def tile_evidentialhead_pa_kernel(tc, x, W1_words, W1_scales, b1, g, beta, out):
         g_all = psum_vec.tile([P, H], BF16, name="g_all")
         beta_all = psum_vec.tile([P, H], BF16, name="beta_all")
         beta_sb = const.tile([P, POOL_COLS], BF16)
+
+        idle_out = psum_acc.tile([P, P], F32, name="idle_out", tag="acc")
+        for i in range(WARM_UP_MATMULS):
+            nc.tensor.matmul(idle_out[:], lhsT=ones[:], rhs=ones[:], start=True, stop=True)
 
         xt, grouped, codes, x_scales, acc = {}, {}, {}, {}, {}
         h, centred, neg_mean, rstd, row_sums, sq_sums, results = {}, {}, {}, {}, {}, {}, {}
@@ -236,11 +241,11 @@ def tile_evidentialhead_pa_kernel(tc, x, W1_words, W1_scales, b1, g, beta, out):
             run(centre_and_gain, j - CENTRE_LAG)
             run(gpsimd_share, j - CENTRE_LAG)
             run(add_bias, j - BIAS_LAG)
-            run(silu_and_mean, j - SILU_LAG)
-            run(variance, j - VARIANCE_LAG)
-            run(mean, j - SILU_LAG)
             run(group_x, j - GROUP_LAG)
+            run(variance, j - VARIANCE_LAG)
+            run(silu_and_mean, j - SILU_LAG)
             run(reciprocal_std, j - VARIANCE_LAG)
+            run(mean, j - SILU_LAG)
             if j == QUANTISE_LAG:
                 spread_b1()
             if j == SILU_LAG:

@@ -24,18 +24,31 @@ BANK = 512
 HALVES = H // BANK
 WORDS = K_PASS // 2
 
-GROUP_LAG = 1
-QUANTISE_LAG = 2
-MULTIPLY_LAG = 3
-BIAS_LAG = 4
-SILU_LAG = 5
-VARIANCE_LAG = 6
-CENTRE_LAG = 7
-STORE_LAG = 8
+GROUPS = (1, 1, 2, 4, 4, 4)
+BIAS_LAG = 1
+SILU_LAG = 2
+VARIANCE_LAG = 3
+CENTRE_LAG = 4
+STORE_LAG = 5
 WARM_UP_MATMULS = 10
-POOL_COLS = 256
+POOL_COLS = 384
 
 FLOPS = 2 * B * D * H
+
+
+def transpose_step(t):
+    if t < 2:
+        return t
+    return max(t // 2 + 1, t - 3)
+
+
+def plan():
+    groups, first, free = [], 0, 0
+    for size in GROUPS:
+        start = max(free, transpose_step(first + size - 1) + 3)
+        groups.append((first, size, start))
+        first, free = first + size, start + size
+    return groups
 
 
 def tile_evidentialhead_pa_kernel(tc, x, W1_words, W1_scales, b1, g, beta, out):
@@ -46,7 +59,7 @@ def tile_evidentialhead_pa_kernel(tc, x, W1_words, W1_scales, b1, g, beta, out):
     with ExitStack() as ctx:
         const = ctx.enter_context(tc.tile_pool(name="const", bufs=1))
         x_pool = ctx.enter_context(tc.tile_pool(name="x_pool", bufs=1))
-        quant = ctx.enter_context(tc.tile_pool(name="quant", bufs=3))
+        quant = ctx.enter_context(tc.tile_pool(name="quant", bufs=1))
         work = ctx.enter_context(tc.tile_pool(name="work", bufs=4))
         stats = ctx.enter_context(tc.tile_pool(name="stats", bufs=4))
         psum_t = ctx.enter_context(tc.psum_pool(name="psum_t", bufs=2))
@@ -86,7 +99,7 @@ def tile_evidentialhead_pa_kernel(tc, x, W1_words, W1_scales, b1, g, beta, out):
 
         for t in range(1, ROW_TILES):
             nc.sync.dma_start(out=x_sb[t][:], in_=x_rows[:, t, :])
-            if t == MULTIPLY_LAG:
+            if t == 3:
                 for which, vec in enumerate((g, beta)):
                     nc.sync.dma_start(out=norm_rows[0:1, which, :], in_=vec.rearrange("(o n) -> o n", o=1))
 
@@ -100,6 +113,13 @@ def tile_evidentialhead_pa_kernel(tc, x, W1_words, W1_scales, b1, g, beta, out):
             nc.tensor.matmul(idle_out[:], lhsT=ones[:], rhs=ones[:], start=True, stop=True)
 
         xt, grouped, codes, x_scales, acc = {}, {}, {}, {}, {}
+        groups = plan()
+        group_of, multiply_step, quantise_at = {}, {}, {}
+        for k, (first, size, start) in enumerate(groups):
+            quantise_at[start - 1] = k
+            for i in range(size):
+                group_of[first + i] = (k, i)
+                multiply_step[first + i] = start + i
         h, centred, neg_mean, rstd, row_sums, sq_sums, results = {}, {}, {}, {}, {}, {}, {}
 
         def transpose_x(t):
@@ -114,29 +134,33 @@ def tile_evidentialhead_pa_kernel(tc, x, W1_words, W1_scales, b1, g, beta, out):
                     )
 
         def group_x(t):
-            grouped[t] = quant.tile([P, PASSES, P, PACK], BF16, name="grouped", tag="grouped", align_bytes=64)
+            k, i = group_of[t]
+            if i == 0:
+                grouped[k] = quant.tile([P, groups[k][1], PASSES, P, PACK], BF16, name="grouped%d" % k, align_bytes=64)
             nc.scalar.copy(
-                out=grouped[t][:].bitcast(F32),
+                out=grouped[k][:, i, :, :, :].bitcast(F32),
                 in_=xt[t][:].rearrange("p (g u) r -> p g r u", u=2),
             )
 
-        def quantise_x(t):
-            codes[t] = quant.tile([P, PASSES * P], U32, name="codes", tag="codes", align_bytes=64)
-            x_scales[t] = quant.tile([P, PASSES * P], U8, name="x_scales", tag="x_scales", align_bytes=64)
+        def quantise_x(k):
+            size = groups[k][1]
+            codes[k] = quant.tile([P, size * PASSES * P], U32, name="codes%d" % k, align_bytes=64)
+            x_scales[k] = quant.tile([P, size * PASSES * P], U8, name="x_scales%d" % k, align_bytes=64)
             nc.vector.quantize_mx(
-                out=codes[t][:].bitcast(FP8X4),
-                scales=x_scales[t][:],
-                in_=grouped[t][:].rearrange("p g r t -> p (g r t)"),
+                out=codes[k][:].bitcast(FP8X4),
+                scales=x_scales[k][:],
+                in_=grouped[k][:].rearrange("p i g r t -> p (i g r t)"),
             )
 
         def multiply(t):
+            k, i = group_of[t]
             for half in range(HALVES):
                 acc[t, half] = psum_acc.tile([P, BANK], F32, name="acc", tag="acc")
                 for gi in range(PASSES):
                     nc.tensor.matmul_mx(
                         out=acc[t, half][:],
-                        lhsT=codes[t][:, P * gi : P * (gi + 1)].bitcast(FP8X4),
-                        lhsT_scale=x_scales[t][:, P * gi : P * (gi + 1)],
+                        lhsT=codes[k][:, P * (PASSES * i + gi) : P * (PASSES * i + gi + 1)].bitcast(FP8X4),
+                        lhsT_scale=x_scales[k][:, P * (PASSES * i + gi) : P * (PASSES * i + gi + 1)],
                         rhs=w_words[:, gi, 2 * BANK * half : 2 * BANK * (half + 1)].bitcast(FP4X4),
                         rhs_scale=w_scales[:, gi, BANK * half : BANK * (half + 1)],
                         start=(gi == 0),
@@ -231,24 +255,36 @@ def tile_evidentialhead_pa_kernel(tc, x, W1_words, W1_scales, b1, g, beta, out):
             spread(norm_rows[:, 1, :], beta_all)
             nc.scalar.copy(out=beta_sb[:], in_=beta_all[:, H - POOL_COLS : H])
 
+        def tile_at(j, lag):
+            t = j - lag
+            return stage_tiles.get(t, -1)
+
+        stage_tiles = {multiply_step[t]: t for t in range(ROW_TILES)}
+        transpose_at = {}
+        for t in range(ROW_TILES):
+            transpose_at.setdefault(transpose_step(t), []).append(t)
+
         def run(stage, t):
-            if 0 <= t < ROW_TILES:
+            if t >= 0:
                 stage(t)
 
-        for j in range(ROW_TILES + STORE_LAG):
-            run(multiply, j - MULTIPLY_LAG)
-            run(transpose_x, j)
-            run(centre_and_gain, j - CENTRE_LAG)
-            run(gpsimd_share, j - CENTRE_LAG)
-            run(add_bias, j - BIAS_LAG)
-            run(group_x, j - GROUP_LAG)
-            run(variance, j - VARIANCE_LAG)
-            run(silu_and_mean, j - SILU_LAG)
-            run(reciprocal_std, j - VARIANCE_LAG)
-            run(mean, j - SILU_LAG)
-            if j == QUANTISE_LAG:
+        for j in range(groups[-1][2] + groups[-1][1] + STORE_LAG):
+            run(multiply, tile_at(j, 0))
+            for t in transpose_at.get(j, ()):
+                transpose_x(t)
+            run(centre_and_gain, tile_at(j, CENTRE_LAG))
+            run(gpsimd_share, tile_at(j, CENTRE_LAG))
+            run(add_bias, tile_at(j, BIAS_LAG))
+            for t in transpose_at.get(j - 1, ()):
+                group_x(t)
+            run(variance, tile_at(j, VARIANCE_LAG))
+            run(silu_and_mean, tile_at(j, SILU_LAG))
+            run(reciprocal_std, tile_at(j, VARIANCE_LAG))
+            run(mean, tile_at(j, SILU_LAG))
+            if j == 2:
                 spread_b1()
-            if j == SILU_LAG:
+            if j == 5:
                 spread_g_beta()
-            run(quantise_x, j - QUANTISE_LAG)
-            run(scale_shift_store, j - STORE_LAG)
+            if j in quantise_at:
+                quantise_x(quantise_at[j])
+            run(scale_shift_store, tile_at(j, STORE_LAG))

@@ -24,28 +24,29 @@ BANK = 512
 HALVES = H // BANK
 WORDS = K_PASS // 2
 
-GROUPS = (1, 1, 2, 4, 4, 4)
+GROUPS = (1, 1, 2, 2, 2, 4, 4)
+
 BIAS_LAG = 1
 SILU_LAG = 2
-VARIANCE_LAG = 3
+SQUARE_LAG = 3
 CENTRE_LAG = 4
 STORE_LAG = 5
 WARM_UP_MATMULS = 10
-POOL_COLS = 384
+POOL_COLS = 448
+ALONE = 2
+G_STEP, BETA_STEP = 4, 6
 
 FLOPS = 2 * B * D * H
 
 
 def transpose_step(t):
-    if t < 2:
-        return t
-    return max(t // 2 + 1, t - 3)
+    return min(t, max((t + 4) // 2, t - 3))
 
 
 def plan():
     groups, first, free = [], 0, 0
     for size in GROUPS:
-        start = max(free, transpose_step(first + size - 1) + 3)
+        start = max(free, transpose_step(first + size - 1) + 2)
         groups.append((first, size, start))
         first, free = first + size, start + size
     return groups
@@ -60,8 +61,8 @@ def tile_evidentialhead_pa_kernel(tc, x, W1_words, W1_scales, b1, g, beta, out):
         const = ctx.enter_context(tc.tile_pool(name="const", bufs=1))
         x_pool = ctx.enter_context(tc.tile_pool(name="x_pool", bufs=1))
         quant = ctx.enter_context(tc.tile_pool(name="quant", bufs=1))
-        work = ctx.enter_context(tc.tile_pool(name="work", bufs=4))
-        stats = ctx.enter_context(tc.tile_pool(name="stats", bufs=4))
+        work = ctx.enter_context(tc.tile_pool(name="work", bufs=5))
+        stats = ctx.enter_context(tc.tile_pool(name="stats", bufs=6))
         psum_t = ctx.enter_context(tc.psum_pool(name="psum_t", bufs=2))
         psum_acc = ctx.enter_context(tc.psum_pool(name="psum_acc", bufs=4))
         psum_vec = ctx.enter_context(tc.psum_pool(name="psum_vec", bufs=1))
@@ -72,7 +73,7 @@ def tile_evidentialhead_pa_kernel(tc, x, W1_words, W1_scales, b1, g, beta, out):
         nc.scalar.activation(out=warm[:], in_=warm[:], func=ACT.Silu)
         ident = const.tile([P, P], F32)
         make_identity(nc, ident[:])
-        neg_half = const.tile([P, 1], F32)
+        neg_half = const.tile([P, 2], F32)
         nc.gpsimd.memset(neg_half[:], -0.5)
 
         ones = const.tile([P, P], BF16)
@@ -85,23 +86,29 @@ def tile_evidentialhead_pa_kernel(tc, x, W1_words, W1_scales, b1, g, beta, out):
         nc.vector.memset(norm_rows[:].bitcast(I32), 0)
 
         x_sb = [x_pool.tile([P, D], BF16, name="x_sb%d" % t) for t in range(ROW_TILES)]
-        nc.sync.dma_start(out=x_sb[0][:], in_=x_rows[:, 0, :])
 
+        def load_x(t):
+            nc.sync.dma_start(out=x_sb[t][:], in_=x_rows[:, t, :])
+
+        def load_row(target, vec):
+            nc.sync.dma_start(out=target, in_=vec.rearrange("(o n) -> o n", o=1))
+
+        load_x(0)
+        load_row(b1_row[0:1, :], b1)
+        load_x(1)
         w_words = const.tile([P, PASSES, 2 * H], U8, align_bytes=64)
         nc.sync.dma_start(
             out=w_words[:].bitcast(I32), in_=W1_words.bitcast(I32).rearrange("g p n -> p g n")
         )
-        nc.sync.dma_start(out=b1_row[0:1, :], in_=b1.rearrange("(o n) -> o n", o=1))
-
         scale_rows = W1_scales.bitcast(I32).rearrange("g (Q r) n -> r Q g n", r=4)
         for r in range(4):
             nc.sync.dma_start(out=w_scales[r:P:32, :, :].bitcast(I32), in_=scale_rows[r])
-
-        for t in range(1, ROW_TILES):
-            nc.sync.dma_start(out=x_sb[t][:], in_=x_rows[:, t, :])
-            if t == 3:
-                for which, vec in enumerate((g, beta)):
-                    nc.sync.dma_start(out=norm_rows[0:1, which, :], in_=vec.rearrange("(o n) -> o n", o=1))
+        load_x(2)
+        load_x(3)
+        load_row(norm_rows[0:1, 0, :], g)
+        load_row(norm_rows[0:1, 1, :], beta)
+        for t in range(4, ROW_TILES):
+            load_x(t)
 
         b1_all = const.tile([P, H], BF16)
         g_all = psum_vec.tile([P, H], BF16, name="g_all")
@@ -113,14 +120,18 @@ def tile_evidentialhead_pa_kernel(tc, x, W1_words, W1_scales, b1, g, beta, out):
             nc.tensor.matmul(idle_out[:], lhsT=ones[:], rhs=ones[:], start=True, stop=True)
 
         xt, grouped, codes, x_scales, acc = {}, {}, {}, {}, {}
+        h, centred, neg_mean, row_sums, sq_sums, var_eps, rstd, results = {}, {}, {}, {}, {}, {}, {}, {}
+
         groups = plan()
-        group_of, multiply_step, quantise_at = {}, {}, {}
+        group_of, tile_in_step, quantised_in, transposed_in = {}, {}, {}, {}
         for k, (first, size, start) in enumerate(groups):
-            quantise_at[start - 1] = k
+            quantised_in[start - 1] = k
             for i in range(size):
                 group_of[first + i] = (k, i)
-                multiply_step[first + i] = start + i
-        h, centred, neg_mean, rstd, row_sums, sq_sums, results = {}, {}, {}, {}, {}, {}, {}
+                tile_in_step[start + i] = first + i
+        for t in range(ROW_TILES):
+            transposed_in.setdefault(transpose_step(t), []).append(t)
+        last_step = groups[-1][2] + groups[-1][1] + STORE_LAG
 
         def transpose_x(t):
             x_words = x_sb[t][:].bitcast(F32)
@@ -136,16 +147,17 @@ def tile_evidentialhead_pa_kernel(tc, x, W1_words, W1_scales, b1, g, beta, out):
         def group_x(t):
             k, i = group_of[t]
             if i == 0:
-                grouped[k] = quant.tile([P, groups[k][1], PASSES, P, PACK], BF16, name="grouped%d" % k, align_bytes=64)
+                size = groups[k][1]
+                grouped[k] = quant.tile([P, size, PASSES, P, PACK], BF16, name="grouped%d" % k, align_bytes=64)
             nc.scalar.copy(
                 out=grouped[k][:, i, :, :, :].bitcast(F32),
                 in_=xt[t][:].rearrange("p (g u) r -> p g r u", u=2),
             )
 
         def quantise_x(k):
-            size = groups[k][1]
-            codes[k] = quant.tile([P, size * PASSES * P], U32, name="codes%d" % k, align_bytes=64)
-            x_scales[k] = quant.tile([P, size * PASSES * P], U8, name="x_scales%d" % k, align_bytes=64)
+            width = groups[k][1] * PASSES * P
+            codes[k] = quant.tile([P, width], U32, name="codes%d" % k, align_bytes=64)
+            x_scales[k] = quant.tile([P, width], U8, name="x_scales%d" % k, align_bytes=64)
             nc.vector.quantize_mx(
                 out=codes[k][:].bitcast(FP8X4),
                 scales=x_scales[k][:],
@@ -157,10 +169,11 @@ def tile_evidentialhead_pa_kernel(tc, x, W1_words, W1_scales, b1, g, beta, out):
             for half in range(HALVES):
                 acc[t, half] = psum_acc.tile([P, BANK], F32, name="acc", tag="acc")
                 for gi in range(PASSES):
+                    rows = slice(P * (PASSES * i + gi), P * (PASSES * i + gi + 1))
                     nc.tensor.matmul_mx(
                         out=acc[t, half][:],
-                        lhsT=codes[k][:, P * (PASSES * i + gi) : P * (PASSES * i + gi + 1)].bitcast(FP8X4),
-                        lhsT_scale=x_scales[k][:, P * (PASSES * i + gi) : P * (PASSES * i + gi + 1)],
+                        lhsT=codes[k][:, rows].bitcast(FP8X4),
+                        lhsT_scale=x_scales[k][:, rows],
                         rhs=w_words[:, gi, 2 * BANK * half : 2 * BANK * (half + 1)].bitcast(FP4X4),
                         rhs_scale=w_scales[:, gi, BANK * half : BANK * (half + 1)],
                         start=(gi == 0),
@@ -173,28 +186,34 @@ def tile_evidentialhead_pa_kernel(tc, x, W1_words, W1_scales, b1, g, beta, out):
                 cols = slice(BANK * half, BANK * (half + 1))
                 nc.vector.tensor_tensor(out=h[t][:, cols], in0=acc[t, half][:], in1=b1_all[:, cols], op=ALU.add)
 
-        def silu_and_mean(t):
-            row_sum = stats.tile([P, 1], F32, name="row_sum", tag="row_sum")
-            nc.scalar.activation(out=h[t][:], in_=h[t][:], func=ACT.Silu, accum_out=row_sum[:])
-            row_sums[t] = row_sum
+        def silu(t):
+            row_sums[t] = stats.tile([P, 1], F32, name="row_sum", tag="row_sum")
+            nc.scalar.activation(out=h[t][:], in_=h[t][:], func=ACT.Silu, accum_out=row_sums[t][:])
 
         def mean(t):
             neg_mean[t] = stats.tile([P, 1], F32, name="neg_mean", tag="neg_mean")
             nc.scalar.activation(out=neg_mean[t][:], in_=row_sums[t][:], func=ACT.Copy, scale=-1.0 / H)
 
-        def variance(t):
+        def square(t):
             squares = work.tile([P, H], F32, name="squares", tag="squares")
-            sq_sum = stats.tile([P, 1], F32, name="sq_sum", tag="sq_sum")
+            sq_sums[t] = stats.tile([P, 1], F32, name="sq_sum", tag="sq_sum")
             nc.scalar.activation(
-                out=squares[:], in_=h[t][:], func=ACT.Square, bias=neg_mean[t][:], scale=1.0, accum_out=sq_sum[:]
+                out=squares[:], in_=h[t][:], func=ACT.Square, bias=neg_mean[t][:], scale=1.0, accum_out=sq_sums[t][:]
             )
-            sq_sums[t] = sq_sum
+
+        def variance(t):
+            if t % 2 == 0:
+                var_eps[t] = var_eps[t + 1] = stats.tile([P, 2], F32, name="var_eps", tag="var_eps")
+            which = slice(t % 2, t % 2 + 1)
+            nc.scalar.activation(
+                out=var_eps[t][:, which], in_=sq_sums[t][:], func=ACT.Copy, scale=1.0 / H, bias=EPS_LN
+            )
 
         def reciprocal_std(t):
-            var_eps = stats.tile([P, 1], F32, name="var_eps", tag="var_eps")
-            nc.scalar.activation(out=var_eps[:], in_=sq_sums[t][:], func=ACT.Copy, scale=1.0 / H, bias=EPS_LN)
-            rstd[t] = stats.tile([P, 1], F32, name="rstd", tag="rstd")
-            nc.gpsimd.tensor_tensor(out=rstd[t][:], in0=var_eps[:], in1=neg_half[:], op=ALU.pow)
+            if t % 2 == 1:
+                pair = stats.tile([P, 2], F32, name="rstd", tag="rstd")
+                nc.gpsimd.tensor_tensor(out=pair[:], in0=var_eps[t][:], in1=neg_half[:], op=ALU.pow)
+                rstd[t - 1], rstd[t] = pair[:, 0:1], pair[:, 1:2]
 
         def centre_and_gain(t):
             centred[t] = work.tile([P, H], F32, name="centred", tag="centred")
@@ -204,87 +223,72 @@ def tile_evidentialhead_pa_kernel(tc, x, W1_words, W1_scales, b1, g, beta, out):
 
         def gpsimd_share(t):
             results[t] = work.tile([P, H], F32, name="result", tag="result")
-            if t < ROW_TILES - 1:
+            if t < ROW_TILES - ALONE:
                 theirs = slice(H - POOL_COLS, H)
                 scaled = work.tile([P, POOL_COLS], F32, name="scaled", tag="scaled")
                 nc.gpsimd.tensor_scalar(
-                    out=scaled[:], in0=centred[t][:, theirs], scalar1=rstd[t][:], scalar2=0.0, op0=ALU.mult, op1=ALU.add
+                    out=scaled[:], in0=centred[t][:, theirs], scalar1=rstd[t], scalar2=0.0, op0=ALU.mult, op1=ALU.add
                 )
                 nc.gpsimd.tensor_tensor(out=results[t][:, theirs], in0=scaled[:], in1=beta_sb[:], op=ALU.add)
 
-        def scale_shift_store(t):
-            result = results[t]
-            if t < ROW_TILES - 1:
-                mine = slice(0, H - POOL_COLS)
-                nc.vector.scalar_tensor_tensor(
-                    out=result[:, mine],
-                    in0=centred[t][:, mine],
-                    scalar=rstd[t][:],
-                    in1=beta_all[:, mine],
-                    op0=ALU.mult,
-                    op1=ALU.add,
-                )
-                nc.sync.dma_start(out=out_rows[:, t, :], in_=result[:])
+        def scale_and_shift(t, cols):
+            nc.vector.scalar_tensor_tensor(
+                out=results[t][:, cols],
+                in0=centred[t][:, cols],
+                scalar=rstd[t],
+                in1=beta_all[:, cols],
+                op0=ALU.mult,
+                op1=ALU.add,
+            )
+
+        def finish(t):
+            if t < ROW_TILES - ALONE:
+                scale_and_shift(t, slice(0, H - POOL_COLS))
+                nc.sync.dma_start(out=out_rows[:, t, :], in_=results[t][:])
                 return
-            pieces = 2
-            width = H // pieces
-            for piece in range(pieces):
-                cols = slice(width * piece, width * (piece + 1))
-                nc.vector.scalar_tensor_tensor(
-                    out=result[:, cols],
-                    in0=centred[t][:, cols],
-                    scalar=rstd[t][:],
-                    in1=beta_all[:, cols],
-                    op0=ALU.mult,
-                    op1=ALU.add,
-                )
-                nc.sync.dma_start(out=out_rows[:, t, cols], in_=result[:, cols])
+            for half in range(HALVES):
+                cols = slice(BANK * half, BANK * (half + 1))
+                scale_and_shift(t, cols)
+                nc.sync.dma_start(out=out_rows[:, t, cols], in_=results[t][:, cols])
 
         def spread(row, target):
             for half in range(HALVES):
                 cols = slice(BANK * half, BANK * (half + 1))
                 nc.tensor.matmul(target[:, cols], lhsT=ones[:], rhs=row[:, cols], start=True, stop=True)
 
-        def spread_b1():
-            b1_ps = psum_acc.tile([P, H], BF16, name="b1_ps", tag="acc")
-            spread(b1_row, b1_ps)
-            nc.scalar.copy(out=b1_all[:], in_=b1_ps[:])
+        def run(stage, j, lag):
+            if j - lag in tile_in_step:
+                stage(tile_in_step[j - lag])
 
-        def spread_g_beta():
-            spread(norm_rows[:, 0, :], g_all)
-            spread(norm_rows[:, 1, :], beta_all)
-            nc.scalar.copy(out=beta_sb[:], in_=beta_all[:, H - POOL_COLS : H])
+        def run_pairs(stage, j, lag):
+            for earlier, parity in ((1, 0), (0, 1)):
+                t = tile_in_step.get(j - lag - earlier, -1)
+                if t >= 0 and t % 2 == parity:
+                    stage(t)
 
-        def tile_at(j, lag):
-            t = j - lag
-            return stage_tiles.get(t, -1)
-
-        stage_tiles = {multiply_step[t]: t for t in range(ROW_TILES)}
-        transpose_at = {}
-        for t in range(ROW_TILES):
-            transpose_at.setdefault(transpose_step(t), []).append(t)
-
-        def run(stage, t):
-            if t >= 0:
-                stage(t)
-
-        for j in range(groups[-1][2] + groups[-1][1] + STORE_LAG):
-            run(multiply, tile_at(j, 0))
-            for t in transpose_at.get(j, ()):
+        for j in range(last_step + 1):
+            run(multiply, j, 0)
+            for t in transposed_in.get(j, ()):
                 transpose_x(t)
-            run(centre_and_gain, tile_at(j, CENTRE_LAG))
-            run(gpsimd_share, tile_at(j, CENTRE_LAG))
-            run(add_bias, tile_at(j, BIAS_LAG))
-            for t in transpose_at.get(j - 1, ()):
+            if j == 0:
+                b1_ps = psum_acc.tile([P, H], BF16, name="b1_ps", tag="acc")
+                spread(b1_row, b1_ps)
+                nc.vector.tensor_copy(out=b1_all[:], in_=b1_ps[:])
+            run(centre_and_gain, j, CENTRE_LAG)
+            run(mean, j, SILU_LAG + 1)
+            run(variance, j, SQUARE_LAG + 1)
+            run(reciprocal_std, j, SQUARE_LAG + 1)
+            run_pairs(gpsimd_share, j, CENTRE_LAG)
+            run(add_bias, j, BIAS_LAG)
+            run(silu, j, SILU_LAG)
+            for t in transposed_in.get(j - 1, ()):
                 group_x(t)
-            run(variance, tile_at(j, VARIANCE_LAG))
-            run(silu_and_mean, tile_at(j, SILU_LAG))
-            run(reciprocal_std, tile_at(j, VARIANCE_LAG))
-            run(mean, tile_at(j, SILU_LAG))
-            if j == 2:
-                spread_b1()
-            if j == 5:
-                spread_g_beta()
-            if j in quantise_at:
-                quantise_x(quantise_at[j])
-            run(scale_shift_store, tile_at(j, STORE_LAG))
+            run(square, j, SQUARE_LAG)
+            if j in quantised_in:
+                quantise_x(quantised_in[j])
+            if j == G_STEP:
+                spread(norm_rows[:, 0, :], g_all)
+                spread(norm_rows[:, 1, :], beta_all)
+            run_pairs(finish, j, STORE_LAG)
+            if j == BETA_STEP:
+                nc.vector.tensor_copy(out=beta_sb[:], in_=beta_all[:, H - POOL_COLS : H])

@@ -32,8 +32,8 @@ SQUARE_LAG = 3
 CENTRE_LAG = 4
 STORE_LAG = 5
 WARM_UP_MATMULS = 10
-POOL_COLS = 448
-ALONE = 2
+POOL_COLS = 480
+ALONE = 3
 G_STEP, BETA_STEP = 4, 6
 
 FLOPS = 2 * B * D * H
@@ -120,7 +120,8 @@ def tile_evidentialhead_pa_kernel(tc, x, W1_words, W1_scales, b1, g, beta, out):
             nc.tensor.matmul(idle_out[:], lhsT=ones[:], rhs=ones[:], start=True, stop=True)
 
         xt, grouped, codes, x_scales, acc = {}, {}, {}, {}, {}
-        h, centred, neg_mean, row_sums, sq_sums, var_eps, rstd, results = {}, {}, {}, {}, {}, {}, {}, {}
+        h, centred, scaled, results = {}, {}, {}, {}
+        neg_mean, row_sums, sq_sums, var_eps, rstd = {}, {}, {}, {}, {}
 
         groups = plan()
         group_of, tile_in_step, quantised_in, transposed_in = {}, {}, {}, {}
@@ -221,15 +222,24 @@ def tile_evidentialhead_pa_kernel(tc, x, W1_words, W1_scales, b1, g, beta, out):
                 out=centred[t][:], in0=h[t][:], scalar=neg_mean[t][:], in1=g_all[:], op0=ALU.add, op1=ALU.mult
             )
 
-        def gpsimd_share(t):
+        def gpsimd_scale(t):
             results[t] = work.tile([P, H], F32, name="result", tag="result")
             if t < ROW_TILES - ALONE:
-                theirs = slice(H - POOL_COLS, H)
-                scaled = work.tile([P, POOL_COLS], F32, name="scaled", tag="scaled")
+                scaled[t] = work.tile([P, POOL_COLS], F32, name="scaled", tag="scaled")
                 nc.gpsimd.tensor_scalar(
-                    out=scaled[:], in0=centred[t][:, theirs], scalar1=rstd[t], scalar2=0.0, op0=ALU.mult, op1=ALU.add
+                    out=scaled[t][:],
+                    in0=centred[t][:, H - POOL_COLS : H],
+                    scalar1=rstd[t],
+                    scalar2=0.0,
+                    op0=ALU.mult,
+                    op1=ALU.add,
                 )
-                nc.gpsimd.tensor_tensor(out=results[t][:, theirs], in0=scaled[:], in1=beta_sb[:], op=ALU.add)
+
+        def gpsimd_shift(t):
+            if t < ROW_TILES - ALONE:
+                nc.gpsimd.tensor_tensor(
+                    out=results[t][:, H - POOL_COLS : H], in0=scaled[t][:], in1=beta_sb[:], op=ALU.add
+                )
 
         def scale_and_shift(t, cols):
             nc.vector.scalar_tensor_tensor(
@@ -275,15 +285,16 @@ def tile_evidentialhead_pa_kernel(tc, x, W1_words, W1_scales, b1, g, beta, out):
                 spread(b1_row, b1_ps)
                 nc.vector.tensor_copy(out=b1_all[:], in_=b1_ps[:])
             run(centre_and_gain, j, CENTRE_LAG)
-            run(mean, j, SILU_LAG + 1)
-            run(variance, j, SQUARE_LAG + 1)
-            run(reciprocal_std, j, SQUARE_LAG + 1)
-            run_pairs(gpsimd_share, j, CENTRE_LAG)
             run(add_bias, j, BIAS_LAG)
+            run(mean, j, SILU_LAG + 1)
             run(silu, j, SILU_LAG)
+            run(variance, j, SQUARE_LAG + 1)
             for t in transposed_in.get(j - 1, ()):
                 group_x(t)
             run(square, j, SQUARE_LAG)
+            run(reciprocal_std, j, SQUARE_LAG + 1)
+            run_pairs(gpsimd_scale, j, CENTRE_LAG)
+            run_pairs(gpsimd_shift, j, CENTRE_LAG)
             if j in quantised_in:
                 quantise_x(quantised_in[j])
             if j == G_STEP:

@@ -31,12 +31,20 @@ SILU_LAG = 2
 SQUARE_LAG = 3
 CENTRE_LAG = 4
 STORE_LAG = 5
-WARM_UP_MATMULS = 10
-POOL_COLS = 480
+WARM_UP_MATMULS = 16
+POOL_COLS = 512
+POOL_COLS_FIRST = 640
+FIRST = 4
 ALONE = 3
 G_STEP, BETA_STEP = 4, 6
 
 FLOPS = 2 * B * D * H
+
+
+def pool_cols(t):
+    if t < FIRST:
+        return POOL_COLS_FIRST
+    return POOL_COLS if t < ROW_TILES - ALONE else 0
 
 
 def transpose_step(t):
@@ -113,7 +121,7 @@ def tile_evidentialhead_pa_kernel(tc, x, W1_words, W1_scales, b1, g, beta, out):
         b1_all = const.tile([P, H], BF16)
         g_all = psum_vec.tile([P, H], BF16, name="g_all")
         beta_all = psum_vec.tile([P, H], BF16, name="beta_all")
-        beta_sb = const.tile([P, POOL_COLS], BF16)
+        beta_sb = const.tile([P, POOL_COLS_FIRST], BF16)
 
         idle_out = psum_acc.tile([P, P], F32, name="idle_out", tag="acc")
         for i in range(WARM_UP_MATMULS):
@@ -197,18 +205,21 @@ def tile_evidentialhead_pa_kernel(tc, x, W1_words, W1_scales, b1, g, beta, out):
 
         def square(t):
             squares = work.tile([P, H], F32, name="squares", tag="squares")
-            sq_sums[t] = stats.tile([P, 1], F32, name="sq_sum", tag="sq_sum")
+            if t % 2 == 0:
+                sq_sums[t] = sq_sums[t + 1] = stats.tile([P, 2], F32, name="sq_sums", tag="sq_sums")
             nc.scalar.activation(
-                out=squares[:], in_=h[t][:], func=ACT.Square, bias=neg_mean[t][:], scale=1.0, accum_out=sq_sums[t][:]
+                out=squares[:],
+                in_=h[t][:],
+                func=ACT.Square,
+                bias=neg_mean[t][:],
+                scale=1.0,
+                accum_out=sq_sums[t][:, t % 2 : t % 2 + 1],
             )
 
         def variance(t):
-            if t % 2 == 0:
-                var_eps[t] = var_eps[t + 1] = stats.tile([P, 2], F32, name="var_eps", tag="var_eps")
-            which = slice(t % 2, t % 2 + 1)
-            nc.scalar.activation(
-                out=var_eps[t][:, which], in_=sq_sums[t][:], func=ACT.Copy, scale=1.0 / H, bias=EPS_LN
-            )
+            if t % 2 == 1:
+                var_eps[t] = stats.tile([P, 2], F32, name="var_eps", tag="var_eps")
+                nc.scalar.activation(out=var_eps[t][:], in_=sq_sums[t][:], func=ACT.Copy, scale=1.0 / H, bias=EPS_LN)
 
         def reciprocal_std(t):
             if t % 2 == 1:
@@ -224,11 +235,12 @@ def tile_evidentialhead_pa_kernel(tc, x, W1_words, W1_scales, b1, g, beta, out):
 
         def gpsimd_scale(t):
             results[t] = work.tile([P, H], F32, name="result", tag="result")
-            if t < ROW_TILES - ALONE:
-                scaled[t] = work.tile([P, POOL_COLS], F32, name="scaled", tag="scaled")
+            width = pool_cols(t)
+            if width:
+                scaled[t] = work.tile([P, width], F32, name="scaled", tag="scaled")
                 nc.gpsimd.tensor_scalar(
                     out=scaled[t][:],
-                    in0=centred[t][:, H - POOL_COLS : H],
+                    in0=centred[t][:, H - width : H],
                     scalar1=rstd[t],
                     scalar2=0.0,
                     op0=ALU.mult,
@@ -236,9 +248,13 @@ def tile_evidentialhead_pa_kernel(tc, x, W1_words, W1_scales, b1, g, beta, out):
                 )
 
         def gpsimd_shift(t):
-            if t < ROW_TILES - ALONE:
+            width = pool_cols(t)
+            if width:
                 nc.gpsimd.tensor_tensor(
-                    out=results[t][:, H - POOL_COLS : H], in0=scaled[t][:], in1=beta_sb[:], op=ALU.add
+                    out=results[t][:, H - width : H],
+                    in0=scaled[t][:],
+                    in1=beta_sb[:, POOL_COLS_FIRST - width :],
+                    op=ALU.add,
                 )
 
         def scale_and_shift(t, cols):
@@ -252,8 +268,8 @@ def tile_evidentialhead_pa_kernel(tc, x, W1_words, W1_scales, b1, g, beta, out):
             )
 
         def finish(t):
-            if t < ROW_TILES - ALONE:
-                scale_and_shift(t, slice(0, H - POOL_COLS))
+            if pool_cols(t):
+                scale_and_shift(t, slice(0, H - pool_cols(t)))
                 nc.sync.dma_start(out=out_rows[:, t, :], in_=results[t][:])
                 return
             for half in range(HALVES):
@@ -302,4 +318,4 @@ def tile_evidentialhead_pa_kernel(tc, x, W1_words, W1_scales, b1, g, beta, out):
                 spread(norm_rows[:, 1, :], beta_all)
             run_pairs(finish, j, STORE_LAG)
             if j == BETA_STEP:
-                nc.vector.tensor_copy(out=beta_sb[:], in_=beta_all[:, H - POOL_COLS : H])
+                nc.vector.tensor_copy(out=beta_sb[:], in_=beta_all[:, H - POOL_COLS_FIRST : H])

@@ -31,6 +31,7 @@ SILU_LAG = 2
 SQUARE_LAG = 3
 CENTRE_LAG = 4
 STORE_LAG = 5
+VECTOR_COPIES = (2, 3)
 WARM_UP_MATMULS = 16
 POOL_COLS = 512
 POOL_COLS_FIRST = 640
@@ -128,7 +129,7 @@ def tile_evidentialhead_pa_kernel(tc, x, W1_words, W1_scales, b1, g, beta, out):
             nc.tensor.matmul(idle_out[:], lhsT=ones[:], rhs=ones[:], start=True, stop=True)
 
         xt, grouped, codes, x_scales, acc = {}, {}, {}, {}, {}
-        h, centred, scaled, results = {}, {}, {}, {}
+        h, centred, pair_scaled, pair_results, results = {}, {}, {}, {}, {}
         neg_mean, row_sums, sq_sums, var_eps, rstd = {}, {}, {}, {}, {}
 
         groups = plan()
@@ -158,7 +159,8 @@ def tile_evidentialhead_pa_kernel(tc, x, W1_words, W1_scales, b1, g, beta, out):
             if i == 0:
                 size = groups[k][1]
                 grouped[k] = quant.tile([P, size, PASSES, P, PACK], BF16, name="grouped%d" % k, align_bytes=64)
-            nc.scalar.copy(
+            copy = nc.vector.tensor_copy if t in VECTOR_COPIES else nc.scalar.copy
+            copy(
                 out=grouped[k][:, i, :, :, :].bitcast(F32),
                 in_=xt[t][:].rearrange("p (g u) r -> p g r u", u=2),
             )
@@ -234,12 +236,15 @@ def tile_evidentialhead_pa_kernel(tc, x, W1_words, W1_scales, b1, g, beta, out):
             )
 
         def gpsimd_scale(t):
-            results[t] = work.tile([P, H], F32, name="result", tag="result")
+            if t % 2 == 0:
+                pair_results[t] = work.tile([P, 2, H], F32, name="results", tag="results", bufs=4)
+                pair_scaled[t] = work.tile([P, 2, pool_cols(t)], F32, name="scaled", tag="scaled") if pool_cols(t) else None
+                for u in (0, 1):
+                    results[t + u] = pair_results[t][:, u, :]
             width = pool_cols(t)
             if width:
-                scaled[t] = work.tile([P, width], F32, name="scaled", tag="scaled")
                 nc.gpsimd.tensor_scalar(
-                    out=scaled[t][:],
+                    out=pair_scaled[t - t % 2][:, t % 2, :],
                     in0=centred[t][:, H - width : H],
                     scalar1=rstd[t],
                     scalar2=0.0,
@@ -248,12 +253,14 @@ def tile_evidentialhead_pa_kernel(tc, x, W1_words, W1_scales, b1, g, beta, out):
                 )
 
         def gpsimd_shift(t):
-            width = pool_cols(t)
-            if width:
+            first = t - t % 2
+            width = pool_cols(first)
+            if t % 2 == 1 and width:
+                tiles = 2 if pool_cols(t) else 1
                 nc.gpsimd.tensor_tensor(
-                    out=results[t][:, H - width : H],
-                    in0=scaled[t][:],
-                    in1=beta_sb[:, POOL_COLS_FIRST - width :],
+                    out=pair_results[first][:, 0:tiles, H - width : H],
+                    in0=pair_scaled[first][:, 0:tiles, :],
+                    in1=beta_sb[:, POOL_COLS_FIRST - width :].unsqueeze(1).to_broadcast([P, tiles, width]),
                     op=ALU.add,
                 )
 
@@ -270,7 +277,10 @@ def tile_evidentialhead_pa_kernel(tc, x, W1_words, W1_scales, b1, g, beta, out):
         def finish(t):
             if pool_cols(t):
                 scale_and_shift(t, slice(0, H - pool_cols(t)))
-                nc.sync.dma_start(out=out_rows[:, t, :], in_=results[t][:])
+                if t % 2 == 1:
+                    nc.sync.dma_start(out=out_rows[:, t - 1 : t + 1, :], in_=pair_results[t - 1][:])
+                elif not pool_cols(t + 1):
+                    nc.sync.dma_start(out=out_rows[:, t, :], in_=results[t])
                 return
             for half in range(HALVES):
                 cols = slice(BANK * half, BANK * (half + 1))

from contextlib import ExitStack

import concourse.mybir as mybir
from concourse.masks import make_identity

F32 = mybir.dt.float32
BF16 = mybir.dt.bfloat16
I32 = mybir.dt.int32
U32 = mybir.dt.uint32
U8 = mybir.dt.uint8
FP8X4 = mybir.dt.float8_e4m3fn_x4
FP4X4 = mybir.dt.float4_e2m1fn_x4
ACT = mybir.ActivationFunctionType
ALU = mybir.AluOpType

P = 128
B, D, H = 2048, 1024, 1024
EPS_LN = 1e-5
PACK = 4
K_PASS = P * PACK
PASSES = D // K_PASS
ROW_TILES = B // P
BANK = 512
HALVES = H // BANK
WORDS = K_PASS // 2

GROUPS = (1, 1, 2, 2, 2, 4, 4)

BIAS_LAG = 1
SILU_LAG = 2
SQUARE_LAG = 3
CENTRE_LAG = 4
STORE_LAG = 5
VECTOR_COPIES = (2, 3)
WARM_UP_MATMULS = 16
POOL_COLS = 512
POOL_COLS_FIRST = 640
FIRST = 4
ALONE = 3
G_STEP, BETA_STEP = 4, 6

FLOPS = 2 * B * D * H


def pool_cols(t):
    if t < FIRST:
        return POOL_COLS_FIRST
    return POOL_COLS if t < ROW_TILES - ALONE else 0


def transpose_step(t):
    return min(t, max((t + 4) // 2, t - 3))


def plan():
    groups, first, free = [], 0, 0
    for size in GROUPS:
        start = max(free, transpose_step(first + size - 1) + 2)
        groups.append((first, size, start))
        first, free = first + size, start + size
    return groups


def tile_evidentialhead_pa_kernel(tc, x, W1_words, W1_scales, b1, g, beta, out):
    nc = tc.nc
    x_rows = x.rearrange("(p t) d -> p t d", t=ROW_TILES)
    out_rows = out.rearrange("(p t) n -> p t n", t=ROW_TILES)

    with ExitStack() as ctx:
        const = ctx.enter_context(tc.tile_pool(name="const", bufs=1))
        x_pool = ctx.enter_context(tc.tile_pool(name="x_pool", bufs=1))
        quant = ctx.enter_context(tc.tile_pool(name="quant", bufs=1))
        work = ctx.enter_context(tc.tile_pool(name="work", bufs=5))
        stats = ctx.enter_context(tc.tile_pool(name="stats", bufs=6))
        psum_t = ctx.enter_context(tc.psum_pool(name="psum_t", bufs=2))
        psum_acc = ctx.enter_context(tc.psum_pool(name="psum_acc", bufs=4))
        psum_vec = ctx.enter_context(tc.psum_pool(name="psum_vec", bufs=1))
        ctx.enter_context(tc.manual_schedule())

        warm = const.tile([P, 1], F32)
        nc.gpsimd.memset(warm[:], 0.0)
        nc.scalar.activation(out=warm[:], in_=warm[:], func=ACT.Silu)
        ident = const.tile([P, P], F32)
        make_identity(nc, ident[:])
        neg_half = const.tile([P, 2], F32)
        nc.gpsimd.memset(neg_half[:], -0.5)

        ones = const.tile([P, P], BF16)
        nc.vector.memset(ones[:], 1.0)
        b1_row = const.tile([P, H], BF16)
        nc.vector.memset(b1_row[:].bitcast(I32), 0)
        w_scales = const.tile([P, PASSES, H], U8, align_bytes=64)
        nc.vector.memset(w_scales[:].bitcast(I32), 0)
        norm_rows = const.tile([P, 2, H], BF16)
        nc.vector.memset(norm_rows[:].bitcast(I32), 0)

        x_sb = [x_pool.tile([P, D], BF16, name="x_sb%d" % t) for t in range(ROW_TILES)]

        def load_x(t):
            nc.sync.dma_start(out=x_sb[t][:], in_=x_rows[:, t, :])

        def load_row(target, vec):
            nc.sync.dma_start(out=target, in_=vec.rearrange("(o n) -> o n", o=1))

        load_x(0)
        load_row(b1_row[0:1, :], b1)
        load_x(1)
        w_words = const.tile([P, PASSES, 2 * H], U8, align_bytes=64)
        nc.sync.dma_start(
            out=w_words[:].bitcast(I32), in_=W1_words.bitcast(I32).rearrange("g p n -> p g n")
        )
        scale_rows = W1_scales.bitcast(I32).rearrange("g (Q r) n -> r Q g n", r=4)
        for r in range(4):
            nc.sync.dma_start(out=w_scales[r:P:32, :, :].bitcast(I32), in_=scale_rows[r])
        load_x(2)
        load_x(3)
        load_row(norm_rows[0:1, 0, :], g)
        load_row(norm_rows[0:1, 1, :], beta)
        for t in range(4, ROW_TILES):
            load_x(t)

        b1_all = const.tile([P, H], BF16)
        g_all = psum_vec.tile([P, H], BF16, name="g_all")
        beta_all = psum_vec.tile([P, H], BF16, name="beta_all")
        beta_sb = const.tile([P, POOL_COLS_FIRST], BF16)

        idle_out = psum_acc.tile([P, P], F32, name="idle_out", tag="acc")
        for i in range(WARM_UP_MATMULS):
            nc.tensor.matmul(idle_out[:], lhsT=ones[:], rhs=ones[:], start=True, stop=True)

        xt, grouped, codes, x_scales, acc = {}, {}, {}, {}, {}
        h, centred, pair_scaled, pair_results, results = {}, {}, {}, {}, {}
        neg_mean, row_sums, sq_sums, var_eps, rstd = {}, {}, {}, {}, {}

        groups = plan()
        group_of, tile_in_step, quantised_in, transposed_in = {}, {}, {}, {}
        for k, (first, size, start) in enumerate(groups):
            quantised_in[start - 1] = k
            for i in range(size):
                group_of[first + i] = (k, i)
                tile_in_step[start + i] = first + i
        for t in range(ROW_TILES):
            transposed_in.setdefault(transpose_step(t), []).append(t)
        last_step = groups[-1][2] + groups[-1][1] + STORE_LAG

        def transpose_x(t):
            x_words = x_sb[t][:].bitcast(F32)
            xt[t] = psum_t.tile([P, PASSES * 2, P], F32, name="xt", tag="xt")
            for gi in range(PASSES):
                for u in range(2):
                    nc.tensor.transpose(
                        xt[t][:, 2 * gi + u, :],
                        x_words[:, WORDS * gi + u : WORDS * (gi + 1) : 2],
                        ident[:],
                    )

        def group_x(t):
            k, i = group_of[t]
            if i == 0:
                size = groups[k][1]
                grouped[k] = quant.tile([P, size, PASSES, P, PACK], BF16, name="grouped%d" % k, align_bytes=64)
            copy = nc.vector.tensor_copy if t in VECTOR_COPIES else nc.scalar.copy
            copy(
                out=grouped[k][:, i, :, :, :].bitcast(F32),
                in_=xt[t][:].rearrange("p (g u) r -> p g r u", u=2),
            )

        def quantise_x(k):
            width = groups[k][1] * PASSES * P
            codes[k] = quant.tile([P, width], U32, name="codes%d" % k, align_bytes=64)
            x_scales[k] = quant.tile([P, width], U8, name="x_scales%d" % k, align_bytes=64)
            nc.vector.quantize_mx(
                out=codes[k][:].bitcast(FP8X4),
                scales=x_scales[k][:],
                in_=grouped[k][:].rearrange("p i g r t -> p (i g r t)"),
            )

        def multiply(t):
            k, i = group_of[t]
            for half in range(HALVES):
                acc[t, half] = psum_acc.tile([P, BANK], F32, name="acc", tag="acc")
                for gi in range(PASSES):
                    rows = slice(P * (PASSES * i + gi), P * (PASSES * i + gi + 1))
                    nc.tensor.matmul_mx(
                        out=acc[t, half][:],
                        lhsT=codes[k][:, rows].bitcast(FP8X4),
                        lhsT_scale=x_scales[k][:, rows],
                        rhs=w_words[:, gi, 2 * BANK * half : 2 * BANK * (half + 1)].bitcast(FP4X4),
                        rhs_scale=w_scales[:, gi, BANK * half : BANK * (half + 1)],
                        start=(gi == 0),
                        stop=(gi == PASSES - 1),
                    )

        def add_bias(t):
            h[t] = work.tile([P, H], F32, name="h", tag="h")
            for half in range(HALVES):
                cols = slice(BANK * half, BANK * (half + 1))
                nc.vector.tensor_tensor(out=h[t][:, cols], in0=acc[t, half][:], in1=b1_all[:, cols], op=ALU.add)

        def silu(t):
            row_sums[t] = stats.tile([P, 1], F32, name="row_sum", tag="row_sum")
            nc.scalar.activation(out=h[t][:], in_=h[t][:], func=ACT.Silu, accum_out=row_sums[t][:])

        def mean(t):
            neg_mean[t] = stats.tile([P, 1], F32, name="neg_mean", tag="neg_mean")
            nc.scalar.activation(out=neg_mean[t][:], in_=row_sums[t][:], func=ACT.Copy, scale=-1.0 / H)

        def square(t):
            squares = work.tile([P, H], F32, name="squares", tag="squares")
            if t % 2 == 0:
                sq_sums[t] = sq_sums[t + 1] = stats.tile([P, 2], F32, name="sq_sums", tag="sq_sums")
            nc.scalar.activation(
                out=squares[:],
                in_=h[t][:],
                func=ACT.Square,
                bias=neg_mean[t][:],
                scale=1.0,
                accum_out=sq_sums[t][:, t % 2 : t % 2 + 1],
            )

        def variance(t):
            if t % 2 == 1:
                var_eps[t] = stats.tile([P, 2], F32, name="var_eps", tag="var_eps")
                nc.scalar.activation(out=var_eps[t][:], in_=sq_sums[t][:], func=ACT.Copy, scale=1.0 / H, bias=EPS_LN)

        def reciprocal_std(t):
            if t % 2 == 1:
                pair = stats.tile([P, 2], F32, name="rstd", tag="rstd")
                nc.gpsimd.tensor_tensor(out=pair[:], in0=var_eps[t][:], in1=neg_half[:], op=ALU.pow)
                rstd[t - 1], rstd[t] = pair[:, 0:1], pair[:, 1:2]

        def centre_and_gain(t):
            centred[t] = work.tile([P, H], F32, name="centred", tag="centred")
            nc.vector.scalar_tensor_tensor(
                out=centred[t][:], in0=h[t][:], scalar=neg_mean[t][:], in1=g_all[:], op0=ALU.add, op1=ALU.mult
            )

        def gpsimd_scale(t):
            if t % 2 == 0:
                pair_results[t] = work.tile([P, 2, H], F32, name="results", tag="results", bufs=4)
                pair_scaled[t] = work.tile([P, 2, pool_cols(t)], F32, name="scaled", tag="scaled") if pool_cols(t) else None
                for u in (0, 1):
                    results[t + u] = pair_results[t][:, u, :]
            width = pool_cols(t)
            if width:
                nc.gpsimd.tensor_scalar(
                    out=pair_scaled[t - t % 2][:, t % 2, :],
                    in0=centred[t][:, H - width : H],
                    scalar1=rstd[t],
                    scalar2=0.0,
                    op0=ALU.mult,
                    op1=ALU.add,
                )

        def gpsimd_shift(t):
            first = t - t % 2
            width = pool_cols(first)
            if t % 2 == 1 and width:
                tiles = 2 if pool_cols(t) else 1
                nc.gpsimd.tensor_tensor(
                    out=pair_results[first][:, 0:tiles, H - width : H],
                    in0=pair_scaled[first][:, 0:tiles, :],
                    in1=beta_sb[:, POOL_COLS_FIRST - width :].unsqueeze(1).to_broadcast([P, tiles, width]),
                    op=ALU.add,
                )

        def scale_and_shift(t, cols):
            nc.vector.scalar_tensor_tensor(
                out=results[t][:, cols],
                in0=centred[t][:, cols],
                scalar=rstd[t],
                in1=beta_all[:, cols],
                op0=ALU.mult,
                op1=ALU.add,
            )

        def finish(t):
            if pool_cols(t):
                scale_and_shift(t, slice(0, H - pool_cols(t)))
                if t % 2 == 1:
                    nc.sync.dma_start(out=out_rows[:, t - 1 : t + 1, :], in_=pair_results[t - 1][:])
                elif not pool_cols(t + 1):
                    nc.sync.dma_start(out=out_rows[:, t, :], in_=results[t])
                return
            for half in range(HALVES):
                cols = slice(BANK * half, BANK * (half + 1))
                scale_and_shift(t, cols)
                nc.sync.dma_start(out=out_rows[:, t, cols], in_=results[t][:, cols])

        def spread(row, target):
            for half in range(HALVES):
                cols = slice(BANK * half, BANK * (half + 1))
                nc.tensor.matmul(target[:, cols], lhsT=ones[:], rhs=row[:, cols], start=True, stop=True)

        def run(stage, j, lag):
            if j - lag in tile_in_step:
                stage(tile_in_step[j - lag])

        def run_pairs(stage, j, lag):
            for earlier, parity in ((1, 0), (0, 1)):
                t = tile_in_step.get(j - lag - earlier, -1)
                if t >= 0 and t % 2 == parity:
                    stage(t)

        for j in range(last_step + 1):
            run(multiply, j, 0)
            for t in transposed_in.get(j, ()):
                transpose_x(t)
            if j == 0:
                b1_ps = psum_acc.tile([P, H], BF16, name="b1_ps", tag="acc")
                spread(b1_row, b1_ps)
                nc.vector.tensor_copy(out=b1_all[:], in_=b1_ps[:])
            run(centre_and_gain, j, CENTRE_LAG)
            run(add_bias, j, BIAS_LAG)
            run(mean, j, SILU_LAG + 1)
            run(silu, j, SILU_LAG)
            run(variance, j, SQUARE_LAG + 1)
            for t in transposed_in.get(j - 1, ()):
                group_x(t)
            run(square, j, SQUARE_LAG)
            run(reciprocal_std, j, SQUARE_LAG + 1)
            run_pairs(gpsimd_scale, j, CENTRE_LAG)
            run_pairs(gpsimd_shift, j, CENTRE_LAG)
            if j in quantised_in:
                quantise_x(quantised_in[j])
            if j == G_STEP:
                spread(norm_rows[:, 0, :], g_all)
                spread(norm_rows[:, 1, :], beta_all)
            run_pairs(finish, j, STORE_LAG)
            if j == BETA_STEP:
                nc.vector.tensor_copy(out=beta_sb[:], in_=beta_all[:, H - POOL_COLS_FIRST : H])
